import numpy as np
import ml_dtypes


def mxq(x, axis, fmt="e4m3"):
    dtype, down = {"e4m3": (ml_dtypes.float8_e4m3fn, 7), "e5m2": (ml_dtypes.float8_e5m2, 14)}[fmt]
    v = np.moveaxis(np.asarray(x, np.float32).astype(ml_dtypes.bfloat16).astype(np.float64), axis, -1)
    blocks = v.reshape(v.shape[:-1] + (-1, 32))
    amax = np.abs(blocks).max(-1, keepdims=True)
    byte = np.maximum(np.where(amax > 0, np.frexp(amax)[1] - 1 + 127, 0) - down, 1)
    scale = np.exp2(byte - 127.0)
    codes = (blocks / scale).astype(np.float32).astype(dtype).astype(np.float64)
    return np.moveaxis((codes * scale).reshape(v.shape), -1, axis)


WIDE = False


def mx_kscale(k):
    if not WIDE:
        return np.ones(k)
    levels = np.array([10, -10, 5, -5, 0])
    a = np.random.permutation(np.resize(levels, k // 512 * 4)).reshape(k // 512, 4)
    idx = np.arange(k)
    return np.exp2(a[idx // 512, idx % 128 // 32])


BF16 = ml_dtypes.bfloat16


def bf(x):
    return np.asarray(x, np.float32).astype(BF16)


def f64(x):
    return np.asarray(x).astype(np.float64)


B, N, D = 320, 8, 256
NT = 100


def erf(v):
    c = np.clip(v, -6.0, 6.0)
    q = 2.0 * c * c
    acc = np.ones_like(c)
    for n in range(NT, 0, -1):
        acc = 1.0 + acc * q / (2 * n + 1)
    return 2.0 / np.sqrt(np.pi) * c * np.exp(-c * c) * acc


def gelu_erf(v):
    return 0.5 * v * (1.0 + erf(v / np.sqrt(2.0)))


def setup_inputs():
    s = mx_kscale(2 * D)[:D]
    s2 = np.concatenate([s, s])
    return {"x": bf(np.random.standard_normal((B, N, D)) * s),
            "W1": bf(np.random.standard_normal((2 * D, 2 * D)) / np.sqrt(2 * D) / s2[:, None]),
            "b1": bf(np.random.standard_normal(2 * D) * 0.5),
            "W2": bf(np.random.standard_normal((2 * D, D)) / np.sqrt(2 * D)),
            "b2": bf(np.random.standard_normal(D) * 0.3)}


def reference(x, W1, b1, W2, b2):
    x, W1, b1, W2, b2 = f64(x), f64(W1), f64(b1), f64(W2), f64(b2)
    ii, jj = np.tril_indices(N)
    cat = np.concatenate([x[:, ii, :], x[:, jj, :]], axis=-1)
    h = gelu_erf((mxq(cat, 2, "e4m3") @ mxq(W1, 0, "e4m3")) + b1)
    pt = (mxq(h, 2, "e4m3") @ mxq(W2, 0, "e4m3")) + b2
    p = np.zeros((B, N, N, D))
    p[:, ii, jj, :] = pt
    mask = np.triu(np.ones((N, N), dtype=bool), 1)
    w = np.sqrt(np.sum(p * p, axis=-1))
    w = np.where(mask[None, :, :], -1e9, w)
    e = np.exp(w - w.max(-1, keepdims=True))
    w = (e / e.sum(-1, keepdims=True))[..., None]
    return np.sum(w * p, axis=2)

@@ -1,0 +1,284 @@
+from contextlib import ExitStack
+
+import concourse.mybir as mybir
+from concourse.masks import make_identity
+
+F32 = mybir.dt.float32
+BF16 = mybir.dt.bfloat16
+U32 = mybir.dt.uint32
+U8 = mybir.dt.uint8
+I32 = mybir.dt.int32
+FP8X4 = mybir.dt.float8_e4m3fn_x4
+ALU = mybir.AluOpType
+ACT = mybir.ActivationFunctionType
+AX = mybir.AxisListType
+
+P = 128
+NPOS = 8
+D = 256
+HID = 512
+CH = 4
+UNIT = 4
+LOG2E = 1.4426950408889634
+FLOPS = 2 * 11520 * 512 * 512 + 2 * 11520 * 512 * 256
+
+
+def build_rows():
+    rows = []
+    for g in range(2):
+        for i in range(NPOS - 1, -1, -1):
+            js = list(range(0, i + 1, 2)) + list(range(1, i + 1, 2))
+            rows.append({"g": g, "isrc": g, "jsrc": g, "i": i, "js": js, "masked": False, "orow": i})
+    for r in range(3, -1, -1):
+        js = list(range(2 * r + 2))
+        rows.append({"g": 2, "isrc": 3, "jsrc": 2, "i": 2 * r + 1, "js": js, "masked": True, "orow": r})
+    return rows
+
+
+def tile_lpair_t_kernel(tc, x, W1, b1, W2, b2, out):
+    nc = tc.nc
+    rows = build_rows()
+    slots = []
+    for ri, row in enumerate(rows):
+        for idx in range(len(row["js"])):
+            slots.append((ri, idx))
+    n_units = len(slots) // UNIT
+    assert n_units * UNIT == len(slots)
+    units = [slots[u * UNIT:(u + 1) * UNIT] for u in range(n_units)]
+    last_unit = {}
+    for u in range(n_units):
+        for (ri, idx) in units[u]:
+            last_unit[ri] = u
+    pos = {}
+    for u in range(n_units):
+        for k, s in enumerate(units[u]):
+            pos[s] = (u, k)
+
+    with ExitStack() as ctx:
+        keep = ctx.enter_context(tc.tile_pool(name="keep", bufs=1))
+        stage = ctx.enter_context(tc.tile_pool(name="stage", bufs=2))
+        hpool = ctx.enter_context(tc.tile_pool(name="hpool", bufs=3))
+        ppool = ctx.enter_context(tc.tile_pool(name="ppool", bufs=9))
+        zpool = ctx.enter_context(tc.psum_pool(name="zpool", bufs=5))
+        qpool = ctx.enter_context(tc.psum_pool(name="qpool", bufs=3))
+
+        xs = [keep.tile([P, NPOS * D], BF16, name="xs%d" % s) for s in range(4)]
+        w1raw_s = keep.tile([P, CH, HID], BF16, name="w1raw_s")
+        w1raw_n = keep.tile([P, CH, HID], BF16, name="w1raw_n")
+        w2raw = keep.tile([P, CH, D], BF16, name="w2raw")
+        b1b = keep.tile([P, CH], BF16, name="b1b")
+        b2b = keep.tile([P, D], BF16, name="b2b")
+        nc.sync.dma_start(out=xs[0][:], in_=x[0:P].rearrange("b n d -> b (n d)"))
+        nc.sync.dma_start(out=w1raw_s[0:64], in_=W1[256:512, :].rearrange("(p j) w -> p j w", j=CH))
+        nc.sync.dma_start(out=w1raw_s[64:128], in_=W1[0:256, :].rearrange("(p j) w -> p j w", j=CH))
+        nc.sync.dma_start(out=b1b[:], in_=b1.rearrange("(m c) -> m c", c=CH))
+        nc.sync.dma_start(out=w1raw_n[:], in_=W1.rearrange("(p j) w -> p j w", j=CH))
+        nc.sync.dma_start(out=w2raw[:], in_=W2.rearrange("(p j) w -> p j w", j=CH))
+        nc.sync.dma_start(out=b2b[:], in_=b2.partition_broadcast(P))
+        nc.sync.dma_start(out=xs[1][:], in_=x[P:2 * P].rearrange("b n d -> b (n d)"))
+        tail = x[2 * P:2 * P + 64]
+        nc.sync.dma_start(out=xs[2][0:64, :], in_=tail.rearrange("b n d -> b (n d)"))
+        nc.sync.dma_start(out=xs[2][64:128, :], in_=tail.rearrange("b n d -> b (n d)"))
+        nc.sync.dma_start(out=xs[3][0:64, :], in_=tail.rearrange("b n d -> b (n d)"))
+        nc.sync.dma_start(out=xs[3][64:128, D:NPOS * D], in_=tail[:, 0:NPOS - 1, :].rearrange("b n d -> b (n d)"))
+        nc.sync.dma_start(out=xs[3][64:128, 0:D], in_=tail[:, 0, :])
+
+        ident = keep.tile([P, P], F32, name="ident")
+        make_identity(nc, ident[:])
+        half = keep.tile([P, NPOS], F32, name="half")
+        two = keep.tile([P, NPOS], F32, name="two")
+        nc.gpsimd.memset(half[:], 0.5)
+        nc.gpsimd.memset(two[:], 2.0)
+
+        def code_tiles(nm, width):
+            c = keep.tile([P, width], U32, name=nm + "_c", align_bytes=64)
+            s = keep.tile([P, width], U8, name=nm + "_s", align_bytes=64)
+            return (c, s)
+
+        w_e = code_tiles("w_e", HID)
+        w_n = code_tiles("w_n", HID)
+        wi = [code_tiles("wi0", HID), code_tiles("wi1", HID)]
+        wj = [code_tiles("wj0", HID), code_tiles("wj1", HID)]
+        for (c, s) in wi + wj:
+            nc.vector.memset(c[:].bitcast(I32), 0)
+            nc.vector.memset(s[:].bitcast(I32), 0)
+        w2q = code_tiles("w2q", D)
+        xq = [code_tiles("xq%d" % s, HID) for s in range(4)]
+
+        b1f = keep.tile([P, CH], F32, name="b1f")
+        nc.vector.tensor_copy(out=b1f[:], in_=b1b[:])
+        b2f = keep.tile([P, 2, D], F32, name="b2f")
+        for h in range(2):
+            nc.vector.tensor_copy(out=b2f[:, h, :], in_=b2b[:])
+        junk = keep.tile([P, D], BF16, name="junk")
+        otile = [keep.tile([P, NPOS, D], F32, name="o0"), keep.tile([P, NPOS, D], F32, name="o1"),
+                 keep.tile([P, 4, D], F32, name="o2")]
+
+        def xprep_t(s):
+            xw = xs[s][:].bitcast(F32).rearrange("p (m q e) -> p m q e", m=4, e=2)
+            xg = stage.tile([P, 4 * P * CH], BF16, name="xg", align_bytes=64)
+            xgw = xg[:].bitcast(F32).rearrange("p (m r e) -> p m r e", m=4, e=2)
+            for kb in range(2):
+                xt = zpool.tile([P, 2, 2, P], F32, name="xt", tag="z")
+                for bb in range(2):
+                    for e in range(2):
+                        nc.tensor.transpose(xt[:, bb, e, :], xw[:, 2 * kb + bb, :, e], ident[:])
+                nc.scalar.copy(out=xgw[:, 2 * kb:2 * kb + 2, :, :], in_=xt[:].rearrange("p b e r -> p b r e"))
+            return xg
+
+        def xprep_q(s, xg):
+            nc.vector.quantize_mx(out=xq[s][0][:].bitcast(FP8X4), scales=xq[s][1][:], in_=xg[:])
+
+        def w1prep(raw, full, top, bottom):
+            g = stage.tile([P, HID, CH], BF16, name="w1g", align_bytes=64)
+            nc.vector.tensor_copy(out=g[:].rearrange("p (c m) j -> p c m j", c=CH),
+                                  in_=raw[:].rearrange("p j (m c) -> p c m j", c=CH))
+            nc.vector.quantize_mx(out=full[0][:].bitcast(FP8X4), scales=full[1][:],
+                                  in_=g[:].rearrange("p w j -> p (w j)"))
+            for (dst, lo, hi) in ((top, 0, 64), (bottom, 64, 128)):
+                for t in range(2):
+                    nc.vector.tensor_copy(out=dst[t][lo:hi, :].bitcast(I32), in_=full[t][lo:hi, :].bitcast(I32))
+
+        xg0 = xprep_t(0)
+        w1prep(w1raw_s, w_e, wj[0], wi[1])
+        xprep_q(0, xg0)
+        w1prep(w1raw_n, w_n, wi[0], wj[1])
+        w2g = stage.tile([P, D, CH], BF16, name="w2g", align_bytes=64)
+        nc.vector.tensor_copy(out=w2g[:].rearrange("p (c i) t -> p c t i", i=4),
+                              in_=w2raw[:].rearrange("p t (c i) -> p c t i", i=4))
+        nc.vector.quantize_mx(out=w2q[0][:].bitcast(FP8X4), scales=w2q[1][:],
+                              in_=w2g[:].rearrange("p w j -> p (w j)"))
+
+        def mx(reg, w, c, src, blk, start, stop):
+            cols = slice(c * P, (c + 1) * P)
+            bc = slice(blk * P, (blk + 1) * P)
+            nc.tensor.matmul_mx(out=reg, lhsT=w[0][:, cols].bitcast(FP8X4), lhsT_scale=w[1][:, cols],
+                                rhs=xq[src][0][:, bc].bitcast(FP8X4), rhs_scale=xq[src][1][:, bc],
+                                start=start, stop=stop)
+
+        hps = {}
+        hcs = {}
+        qbs = {}
+        pts = {}
+        small = {}
+
+        def stage1(u):
+            hp = hpool.tile([P, CH, UNIT * P], BF16, name="hp")
+            hps[u] = hp
+            for c in range(CH):
+                z = zpool.tile([P, UNIT * P], F32, name="z", tag="z")
+                for k, (ri, idx) in enumerate(units[u]):
+                    row = rows[ri]
+                    i = row["i"]
+                    j = row["js"][idx]
+                    reg = z[:, k * P:(k + 1) * P]
+                    if row["isrc"] == row["jsrc"] and i == j + 1 and j % 2 == 0:
+                        mx(reg, w_e, c, row["isrc"], j // 2, True, True)
+                    else:
+                        mx(reg, wi[i % 2], c, row["isrc"], i // 2, True, False)
+                        mx(reg, wj[j % 2], c, row["jsrc"], j // 2, False, True)
+                nc.scalar.activation(out=hp[:, c, :], in_=z[:], func=ACT.Gelu, bias=b1f[:, c:c + 1], scale=1.0)
+
+        def regroup_quant(u):
+            hp = hps[u]
+            hg = hpool.tile([P, UNIT * P, CH], BF16, name="hg", align_bytes=64)
+            nc.vector.tensor_copy(out=hg[:].rearrange("p (c i) t -> p c t i", i=4),
+                                  in_=hp[:].rearrange("p t (c i) -> p c t i", i=4))
+            hc = hpool.tile([P, UNIT * P], U32, name="hc", align_bytes=64)
+            hs = hpool.tile([P, UNIT * P], U8, name="hs", align_bytes=64)
+            nc.vector.quantize_mx(out=hc[:].bitcast(FP8X4), scales=hs[:], in_=hg[:].rearrange("p r t -> p (r t)"))
+            hcs[u] = (hc, hs)
+
+        def stage2(u):
+            (hc, hs) = hcs[u]
+            qbs[u] = []
+            for kk in range(2):
+                qb = qpool.tile([P, 2, D], F32, name="qb")
+                for h in range(2):
+                    cols = slice((2 * kk + h) * P, (2 * kk + h + 1) * P)
+                    nc.tensor.matmul_mx(out=qb[:, h, :], lhsT=hc[:, cols].bitcast(FP8X4), lhsT_scale=hs[:, cols],
+                                        rhs=w2q[0][:].bitcast(FP8X4), rhs_scale=w2q[1][:], start=True, stop=True)
+                qbs[u].append(qb)
+
+        def sm_tile(ri, nm, width):
+            t = keep.tile([P, width], F32, name="%s_%d" % (nm, ri))
+            small[(ri, nm)] = t
+            return t
+
+        def evac(u):
+            pt = ppool.tile([P, UNIT, D], F32, name="pt")
+            pts[u] = pt
+            for kk in range(2):
+                nc.vector.tensor_tensor(out=pt[:, 2 * kk:2 * kk + 2, :], in0=qbs[u][kk][:], in1=b2f[:], op=ALU.add)
+            for k, (ri, idx) in enumerate(units[u]):
+                if idx == 0:
+                    sm_tile(ri, "n2", NPOS)
+                nc.scalar.activation(out=junk[:], in_=pt[:, k, :], func=ACT.Square,
+                                     accum_out=small[(ri, "n2")][:, idx:idx + 1])
+
+        def sm_a(ri):
+            n = len(rows[ri]["js"])
+            nrm = sm_tile(ri, "nrm", NPOS)
+            nc.gpsimd.tensor_tensor(out=nrm[:, 0:n], in0=small[(ri, "n2")][:, 0:n], in1=half[:, 0:n], op=ALU.pow)
+            if rows[ri]["masked"]:
+                nc.gpsimd.memset(nrm[64:128, n - 1:n], 0.0)
+
+        def sm_b(ri):
+            n = len(rows[ri]["js"])
+            nrm = small[(ri, "nrm")]
+            mxv = sm_tile(ri, "mx", 1)
+            nc.vector.tensor_reduce(out=mxv[:], in_=nrm[:, 0:n], axis=AX.X, op=ALU.max)
+            dd = sm_tile(ri, "dd", NPOS)
+            nc.vector.tensor_scalar(out=dd[:, 0:n], in0=nrm[:, 0:n], scalar1=mxv[:, 0:1], scalar2=LOG2E,
+                                    op0=ALU.subtract, op1=ALU.mult)
+            ee = sm_tile(ri, "ee", NPOS)
+            nc.gpsimd.tensor_tensor(out=ee[:, 0:n], in0=two[:, 0:n], in1=dd[:, 0:n], op=ALU.pow)
+            if rows[ri]["masked"]:
+                nc.gpsimd.memset(ee[64:128, n - 1:n], 0.0)
+
+        def sm_c(ri):
+            row = rows[ri]
+            n = len(row["js"])
+            ee = small[(ri, "ee")]
+            sv = sm_tile(ri, "sv", 1)
+            nc.vector.tensor_reduce(out=sv[:], in_=ee[:, 0:n], axis=AX.X, op=ALU.add)
+            rv = sm_tile(ri, "rv", 1)
+            nc.vector.reciprocal(out=rv[:], in_=sv[:])
+            aa = sm_tile(ri, "aa", NPOS)
+            nc.vector.tensor_scalar(out=aa[:, 0:n], in0=ee[:, 0:n], scalar1=rv[:, 0:1], scalar2=None, op0=ALU.mult)
+            acc = otile[row["g"]][:, row["orow"], :]
+            for idx in range(n):
+                (u, k) = pos[(ri, idx)]
+                src = pts[u][:, k, :]
+                if idx == 0:
+                    nc.vector.tensor_scalar(out=acc, in0=src, scalar1=aa[:, 0:1], scalar2=None, op0=ALU.mult)
+                else:
+                    nc.vector.scalar_tensor_tensor(out=acc, in0=src, scalar=aa[:, idx:idx + 1], in1=acc,
+                                                   op0=ALU.mult, op1=ALU.add)
+            g = row["g"]
+            if g < 2:
+                nc.sync.dma_start(out=out[g * P:(g + 1) * P, row["i"], :], in_=acc)
+            else:
+                r = row["orow"]
+                nc.sync.dma_start(out=out[2 * P:2 * P + 64, 2 * r + 1, :], in_=otile[2][0:64, r, :])
+                nc.sync.dma_start(out=out[2 * P:2 * P + 64, 2 * r, :], in_=otile[2][64:128, r, :])
+
+        later_x = {2: 1, 7: 2, 9: 3}
+        for t in range(n_units + 5):
+            if t < n_units:
+                stage1(t)
+            if t in later_x:
+                s = later_x[t]
+                xprep_q(s, xprep_t(s))
+            if 0 <= t - 2 < n_units:
+                evac(t - 2)
+            if 0 <= t - 1 < n_units:
+                regroup_quant(t - 1)
+                stage2(t - 1)
+            for ri in range(len(rows)):
+                if last_unit[ri] == t - 2:
+                    sm_a(ri)
+                if last_unit[ri] == t - 3:
+                    sm_b(ri)
+                if last_unit[ri] == t - 4:
+                    sm_c(ri)

@@ -22,43 +22,57 @@ UNIT = 4
 LOG2E = 1.4426950408889634
 FLOPS = 2 * 11520 * 512 * 512 + 2 * 11520 * 512 * 256
 
+PBUFS = 17
+E3CAP = 6
+R_ON_SCALAR = ()
+PINNED = True
+LAG_B = 5
+LAG_C = 7
 
-def build_rows():
-    rows = []
-    for g in range(2):
-        for i in range(NPOS - 1, -1, -1):
-            js = list(range(0, i + 1, 2)) + list(range(1, i + 1, 2))
-            rows.append({"g": g, "isrc": g, "jsrc": g, "i": i, "js": js, "masked": False, "orow": i})
-    for r in range(3, -1, -1):
-        js = list(range(2 * r + 2))
-        rows.append({"g": 2, "isrc": 3, "jsrc": 2, "i": 2 * r + 1, "js": js, "masked": True, "orow": r})
-    return rows
+
+def full_row(g, i):
+    js = list(range(0, i + 1, 2)) + list(range(1, i + 1, 2))
+    return {"g": g, "isrc": g, "jsrc": g, "i": i, "js": js, "orow": i}
+
+
+def build_batches():
+    batches = []
+    for i in (7, 6, 5):
+        batches.append({"rows": [full_row(0, i), full_row(1, i)], "masked": False, "direct": False})
+    for r in (3, 2, 1, 0):
+        row = {"g": 2, "isrc": 3, "jsrc": 2, "i": 2 * r + 1, "js": list(range(2 * r + 2)), "orow": r}
+        batches.append({"rows": [row], "masked": True, "direct": False})
+    for i in (4, 3, 2, 1):
+        batches.append({"rows": [full_row(0, i), full_row(1, i)], "masked": False, "direct": False})
+    batches.append({"rows": [full_row(0, 0), full_row(1, 0)], "masked": False, "direct": True})
+    return batches
 
 
 def tile_lpair_t_kernel(tc, x, W1, b1, W2, b2, out):
     nc = tc.nc
-    rows = build_rows()
+    batches = build_batches()
     slots = []
-    for ri, row in enumerate(rows):
-        for idx in range(len(row["js"])):
-            slots.append((ri, idx))
+    for bi, bt in enumerate(batches):
+        for rr, row in enumerate(bt["rows"]):
+            for idx in range(len(row["js"])):
+                slots.append((bi, rr, idx))
     n_units = len(slots) // UNIT
     assert n_units * UNIT == len(slots)
     units = [slots[u * UNIT:(u + 1) * UNIT] for u in range(n_units)]
     last_unit = {}
-    for u in range(n_units):
-        for (ri, idx) in units[u]:
-            last_unit[ri] = u
     pos = {}
     for u in range(n_units):
         for k, s in enumerate(units[u]):
+            last_unit[s[0]] = u
             pos[s] = (u, k)
 
     with ExitStack() as ctx:
+        if PINNED:
+            ctx.enter_context(tc.manual_schedule())
         keep = ctx.enter_context(tc.tile_pool(name="keep", bufs=1))
         stage = ctx.enter_context(tc.tile_pool(name="stage", bufs=2))
         hpool = ctx.enter_context(tc.tile_pool(name="hpool", bufs=3))
-        ppool = ctx.enter_context(tc.tile_pool(name="ppool", bufs=9))
+        ppool = ctx.enter_context(tc.tile_pool(name="ppool", bufs=PBUFS))
         zpool = ctx.enter_context(tc.psum_pool(name="zpool", bufs=5))
         qpool = ctx.enter_context(tc.psum_pool(name="qpool", bufs=3))
 
@@ -73,9 +87,9 @@ def tile_lpair_t_kernel(tc, x, W1, b1, W2, b2, out):
         nc.sync.dma_start(out=w1raw_s[64:128], in_=W1[0:256, :].rearrange("(p j) w -> p j w", j=CH))
         nc.sync.dma_start(out=b1b[:], in_=b1.rearrange("(m c) -> m c", c=CH))
         nc.sync.dma_start(out=w1raw_n[:], in_=W1.rearrange("(p j) w -> p j w", j=CH))
+        nc.sync.dma_start(out=xs[1][:], in_=x[P:2 * P].rearrange("b n d -> b (n d)"))
         nc.sync.dma_start(out=w2raw[:], in_=W2.rearrange("(p j) w -> p j w", j=CH))
         nc.sync.dma_start(out=b2b[:], in_=b2.partition_broadcast(P))
-        nc.sync.dma_start(out=xs[1][:], in_=x[P:2 * P].rearrange("b n d -> b (n d)"))
         tail = x[2 * P:2 * P + 64]
         nc.sync.dma_start(out=xs[2][0:64, :], in_=tail.rearrange("b n d -> b (n d)"))
         nc.sync.dma_start(out=xs[2][64:128, :], in_=tail.rearrange("b n d -> b (n d)"))
@@ -85,8 +99,8 @@ def tile_lpair_t_kernel(tc, x, W1, b1, W2, b2, out):
 
         ident = keep.tile([P, P], F32, name="ident")
         make_identity(nc, ident[:])
-        half = keep.tile([P, NPOS], F32, name="half")
-        two = keep.tile([P, NPOS], F32, name="two")
+        half = keep.tile([P, 2, NPOS], F32, name="half")
+        two = keep.tile([P, 2, NPOS], F32, name="two")
         nc.gpsimd.memset(half[:], 0.5)
         nc.gpsimd.memset(two[:], 2.0)
 
@@ -99,18 +113,17 @@ def tile_lpair_t_kernel(tc, x, W1, b1, W2, b2, out):
         w_n = code_tiles("w_n", HID)
         wi = [code_tiles("wi0", HID), code_tiles("wi1", HID)]
         wj = [code_tiles("wj0", HID), code_tiles("wj1", HID)]
+        w2q = code_tiles("w2q", D)
+        xq = [code_tiles("xq%d" % s, HID) for s in range(4)]
+        warm = keep.tile([P, 1], F32, name="warm")
+        nc.vector.memset(warm[:], 0.0)
+        junk = keep.tile([P, D], BF16, name="junk")
+        nc.scalar.activation(out=junk[:, 0:1], in_=warm[:], func=ACT.Gelu)
         for (c, s) in wi + wj:
             nc.vector.memset(c[:].bitcast(I32), 0)
             nc.vector.memset(s[:].bitcast(I32), 0)
-        w2q = code_tiles("w2q", D)
-        xq = [code_tiles("xq%d" % s, HID) for s in range(4)]
-
         b1f = keep.tile([P, CH], F32, name="b1f")
-        nc.vector.tensor_copy(out=b1f[:], in_=b1b[:])
         b2f = keep.tile([P, 2, D], F32, name="b2f")
-        for h in range(2):
-            nc.vector.tensor_copy(out=b2f[:, h, :], in_=b2b[:])
-        junk = keep.tile([P, D], BF16, name="junk")
         otile = [keep.tile([P, NPOS, D], F32, name="o0"), keep.tile([P, NPOS, D], F32, name="o1"),
                  keep.tile([P, 4, D], F32, name="o2")]
 
@@ -129,10 +142,13 @@ def tile_lpair_t_kernel(tc, x, W1, b1, W2, b2, out):
         def xprep_q(s, xg):
             nc.vector.quantize_mx(out=xq[s][0][:].bitcast(FP8X4), scales=xq[s][1][:], in_=xg[:])
 
-        def w1prep(raw, full, top, bottom):
+        def w1_regroup(eng_copy, raw):
             g = stage.tile([P, HID, CH], BF16, name="w1g", align_bytes=64)
-            nc.vector.tensor_copy(out=g[:].rearrange("p (c m) j -> p c m j", c=CH),
-                                  in_=raw[:].rearrange("p j (m c) -> p c m j", c=CH))
+            eng_copy(out=g[:].rearrange("p (c m) j -> p c m j", c=CH),
+                     in_=raw[:].rearrange("p j (m c) -> p c m j", c=CH))
+            return g
+
+        def w1_quant(g, full, top, bottom):
             nc.vector.quantize_mx(out=full[0][:].bitcast(FP8X4), scales=full[1][:],
                                   in_=g[:].rearrange("p w j -> p (w j)"))
             for (dst, lo, hi) in ((top, 0, 64), (bottom, 64, 128)):
@@ -140,14 +156,21 @@ def tile_lpair_t_kernel(tc, x, W1, b1, W2, b2, out):
                     nc.vector.tensor_copy(out=dst[t][lo:hi, :].bitcast(I32), in_=full[t][lo:hi, :].bitcast(I32))
 
         xg0 = xprep_t(0)
-        w1prep(w1raw_s, w_e, wj[0], wi[1])
+        g_s = w1_regroup(nc.vector.tensor_copy, w1raw_s)
+        g_n = w1_regroup(nc.scalar.copy, w1raw_n)
+        nc.vector.tensor_copy(out=b1f[:], in_=b1b[:])
+        w1_quant(g_s, w_e, wj[0], wi[1])
         xprep_q(0, xg0)
-        w1prep(w1raw_n, w_n, wi[0], wj[1])
+        xg1 = xprep_t(1)
+        w1_quant(g_n, w_n, wi[0], wj[1])
         w2g = stage.tile([P, D, CH], BF16, name="w2g", align_bytes=64)
         nc.vector.tensor_copy(out=w2g[:].rearrange("p (c i) t -> p c t i", i=4),
                               in_=w2raw[:].rearrange("p t (c i) -> p c t i", i=4))
+        xprep_q(1, xg1)
         nc.vector.quantize_mx(out=w2q[0][:].bitcast(FP8X4), scales=w2q[1][:],
                               in_=w2g[:].rearrange("p w j -> p (w j)"))
+        for h in range(2):
+            nc.vector.tensor_copy(out=b2f[:, h, :], in_=b2b[:])
 
         def mx(reg, w, c, src, blk, start, stop):
             cols = slice(c * P, (c + 1) * P)
@@ -157,18 +180,21 @@ def tile_lpair_t_kernel(tc, x, W1, b1, W2, b2, out):
                                 start=start, stop=stop)
 
         hps = {}
+        hgs = {}
         hcs = {}
         qbs = {}
         pts = {}
         small = {}
+        left = {}
+        state = {"rr": 0, "chains": []}
 
         def stage1(u):
             hp = hpool.tile([P, CH, UNIT * P], BF16, name="hp")
             hps[u] = hp
             for c in range(CH):
                 z = zpool.tile([P, UNIT * P], F32, name="z", tag="z")
-                for k, (ri, idx) in enumerate(units[u]):
-                    row = rows[ri]
+                for k, (bi, rr, idx) in enumerate(units[u]):
+                    row = batches[bi]["rows"][rr]
                     i = row["i"]
                     j = row["js"][idx]
                     reg = z[:, k * P:(k + 1) * P]
@@ -179,14 +205,17 @@ def tile_lpair_t_kernel(tc, x, W1, b1, W2, b2, out):
                         mx(reg, wj[j % 2], c, row["jsrc"], j // 2, False, True)
                 nc.scalar.activation(out=hp[:, c, :], in_=z[:], func=ACT.Gelu, bias=b1f[:, c:c + 1], scale=1.0)
 
-        def regroup_quant(u):
-            hp = hps[u]
+        def regroup(u):
             hg = hpool.tile([P, UNIT * P, CH], BF16, name="hg", align_bytes=64)
-            nc.vector.tensor_copy(out=hg[:].rearrange("p (c i) t -> p c t i", i=4),
-                                  in_=hp[:].rearrange("p t (c i) -> p c t i", i=4))
+            hgs[u] = hg
+            cp = nc.scalar.copy if u in R_ON_SCALAR else nc.vector.tensor_copy
+            cp(out=hg[:].rearrange("p (c i) t -> p c t i", i=4), in_=hps[u][:].rearrange("p t (c i) -> p c t i", i=4))
+
+        def quant(u):
             hc = hpool.tile([P, UNIT * P], U32, name="hc", align_bytes=64)
             hs = hpool.tile([P, UNIT * P], U8, name="hs", align_bytes=64)
-            nc.vector.quantize_mx(out=hc[:].bitcast(FP8X4), scales=hs[:], in_=hg[:].rearrange("p r t -> p (r t)"))
+            nc.vector.quantize_mx(out=hc[:].bitcast(FP8X4), scales=hs[:],
+                                  in_=hgs[u][:].rearrange("p r t -> p (r t)"))
             hcs[u] = (hc, hs)
 
         def stage2(u):
@@ -200,85 +229,140 @@ def tile_lpair_t_kernel(tc, x, W1, b1, W2, b2, out):
                                         rhs=w2q[0][:].bitcast(FP8X4), rhs_scale=w2q[1][:], start=True, stop=True)
                 qbs[u].append(qb)
 
-        def sm_tile(ri, nm, width):
-            t = keep.tile([P, width], F32, name="%s_%d" % (nm, ri))
-            small[(ri, nm)] = t
+        def sm_tile(bi, nm, width):
+            t = keep.tile([P, 2, width], F32, name="%s_%d" % (nm, bi))
+            small[(bi, nm)] = t
             return t
 
-        def evac(u):
-            pt = ppool.tile([P, UNIT, D], F32, name="pt")
-            pts[u] = pt
-            for kk in range(2):
-                nc.vector.tensor_tensor(out=pt[:, 2 * kk:2 * kk + 2, :], in0=qbs[u][kk][:], in1=b2f[:], op=ALU.add)
-            for k, (ri, idx) in enumerate(units[u]):
-                if idx == 0:
-                    sm_tile(ri, "n2", NPOS)
-                nc.scalar.activation(out=junk[:], in_=pt[:, k, :], func=ACT.Square,
-                                     accum_out=small[(ri, "n2")][:, idx:idx + 1])
-
-        def sm_a(ri):
-            n = len(rows[ri]["js"])
-            nrm = sm_tile(ri, "nrm", NPOS)
-            nc.gpsimd.tensor_tensor(out=nrm[:, 0:n], in0=small[(ri, "n2")][:, 0:n], in1=half[:, 0:n], op=ALU.pow)
-            if rows[ri]["masked"]:
-                nc.gpsimd.memset(nrm[64:128, n - 1:n], 0.0)
-
-        def sm_b(ri):
-            n = len(rows[ri]["js"])
-            nrm = small[(ri, "nrm")]
-            mxv = sm_tile(ri, "mx", 1)
-            nc.vector.tensor_reduce(out=mxv[:], in_=nrm[:, 0:n], axis=AX.X, op=ALU.max)
-            dd = sm_tile(ri, "dd", NPOS)
-            nc.vector.tensor_scalar(out=dd[:, 0:n], in0=nrm[:, 0:n], scalar1=mxv[:, 0:1], scalar2=LOG2E,
-                                    op0=ALU.subtract, op1=ALU.mult)
-            ee = sm_tile(ri, "ee", NPOS)
-            nc.gpsimd.tensor_tensor(out=ee[:, 0:n], in0=two[:, 0:n], in1=dd[:, 0:n], op=ALU.pow)
-            if rows[ri]["masked"]:
-                nc.gpsimd.memset(ee[64:128, n - 1:n], 0.0)
-
-        def sm_c(ri):
-            row = rows[ri]
-            n = len(row["js"])
-            ee = small[(ri, "ee")]
-            sv = sm_tile(ri, "sv", 1)
-            nc.vector.tensor_reduce(out=sv[:], in_=ee[:, 0:n], axis=AX.X, op=ALU.add)
-            rv = sm_tile(ri, "rv", 1)
-            nc.vector.reciprocal(out=rv[:], in_=sv[:])
-            aa = sm_tile(ri, "aa", NPOS)
-            nc.vector.tensor_scalar(out=aa[:, 0:n], in0=ee[:, 0:n], scalar1=rv[:, 0:1], scalar2=None, op0=ALU.mult)
+        def e3_step():
+            chains = state["chains"]
+            if len(chains) == 0:
+                return False
+            state["rr"] = (state["rr"] + 1) % len(chains)
+            ch = chains[state["rr"]]
+            (bi, rr, idx) = (ch[0], ch[1], ch[2])
+            row = batches[bi]["rows"][rr]
+            aa = small[(bi, "aa")]
+            (u, k) = pos[(bi, rr, idx)]
             acc = otile[row["g"]][:, row["orow"], :]
-            for idx in range(n):
-                (u, k) = pos[(ri, idx)]
-                src = pts[u][:, k, :]
-                if idx == 0:
-                    nc.vector.tensor_scalar(out=acc, in0=src, scalar1=aa[:, 0:1], scalar2=None, op0=ALU.mult)
-                else:
-                    nc.vector.scalar_tensor_tensor(out=acc, in0=src, scalar=aa[:, idx:idx + 1], in1=acc,
-                                                   op0=ALU.mult, op1=ALU.add)
-            g = row["g"]
-            if g < 2:
-                nc.sync.dma_start(out=out[g * P:(g + 1) * P, row["i"], :], in_=acc)
+            if idx == 0:
+                nc.vector.tensor_scalar(out=acc, in0=pts[u][:, k, :], scalar1=aa[:, rr, 0:1], scalar2=None,
+                                        op0=ALU.mult)
             else:
-                r = row["orow"]
-                nc.sync.dma_start(out=out[2 * P:2 * P + 64, 2 * r + 1, :], in_=otile[2][0:64, r, :])
-                nc.sync.dma_start(out=out[2 * P:2 * P + 64, 2 * r, :], in_=otile[2][64:128, r, :])
+                nc.vector.scalar_tensor_tensor(out=acc, in0=pts[u][:, k, :], scalar=aa[:, rr, idx:idx + 1], in1=acc,
+                                               op0=ALU.mult, op1=ALU.add)
+            left[u] -= 1
+            ch[2] += 1
+            if ch[2] == len(row["js"]):
+                state["chains"] = [c for c in chains if c[2] < len(batches[c[0]]["rows"][c[1]]["js"])]
+                g = row["g"]
+                if g < 2:
+                    nc.sync.dma_start(out=out[g * P:(g + 1) * P, row["i"], :], in_=acc)
+                else:
+                    r = row["orow"]
+                    nc.sync.dma_start(out=out[2 * P:2 * P + 64, 2 * r + 1, :], in_=otile[2][0:64, r, :])
+                    nc.sync.dma_start(out=out[2 * P:2 * P + 64, 2 * r, :], in_=otile[2][64:128, r, :])
+            return True
 
-        later_x = {2: 1, 7: 2, 9: 3}
-        for t in range(n_units + 5):
+        def e3_steps(n):
+            done = 0
+            while done < n and e3_step():
+                done += 1
+            return done
+
+        def evac_alloc(u):
+            if u - PBUFS in left:
+                while left[u - PBUFS] > 0:
+                    assert e3_step()
+            pts[u] = ppool.tile([P, UNIT, D], F32, name="pt")
+            left[u] = UNIT
+
+        def evac(u, kk):
+            nc.vector.tensor_tensor(out=pts[u][:, 2 * kk:2 * kk + 2, :], in0=qbs[u][kk][:], in1=b2f[:], op=ALU.add)
+
+        def squares(u):
+            for k, (bi, rr, idx) in enumerate(units[u]):
+                row = batches[bi]["rows"][rr]
+                if batches[bi]["direct"]:
+                    g = row["g"]
+                    nc.sync.dma_start(out=out[g * P:(g + 1) * P, row["i"], :], in_=pts[u][:, k, :])
+                    left[u] -= 1
+                    continue
+                if (bi, "n2") not in small:
+                    sm_tile(bi, "n2", NPOS)
+                nc.scalar.activation(out=junk[:], in_=pts[u][:, k, :], func=ACT.Square, scale=LOG2E,
+                                     accum_out=small[(bi, "n2")][:, rr, idx:idx + 1])
+
+        def dims(bi):
+            return (len(batches[bi]["rows"]), len(batches[bi]["rows"][0]["js"]))
+
+        def sm_a(bi):
+            (nr, n) = dims(bi)
+            nrm = sm_tile(bi, "nrm", NPOS)
+            nc.gpsimd.tensor_tensor(out=nrm[:, 0:nr, 0:n], in0=small[(bi, "n2")][:, 0:nr, 0:n],
+                                    in1=half[:, 0:nr, 0:n], op=ALU.pow)
+            if batches[bi]["masked"]:
+                nc.gpsimd.memset(nrm[64:128, 0, n - 1:n], 0.0)
+
+        def sm_b(bi):
+            (nr, n) = dims(bi)
+            nrm = small[(bi, "nrm")]
+            mxv = sm_tile(bi, "mx", 1)
+            nc.vector.tensor_reduce(out=mxv[:, 0:nr, 0], in_=nrm[:, 0:nr, 0:n], axis=AX.X, op=ALU.max)
+            dd = sm_tile(bi, "dd", NPOS)
+            nc.vector.tensor_tensor(out=dd[:, 0:nr, 0:n], in0=nrm[:, 0:nr, 0:n],
+                                    in1=mxv[:, 0:nr, :].to_broadcast([P, nr, n]), op=ALU.subtract)
+            ee = sm_tile(bi, "ee", NPOS)
+            nc.gpsimd.tensor_tensor(out=ee[:, 0:nr, 0:n], in0=two[:, 0:nr, 0:n], in1=dd[:, 0:nr, 0:n], op=ALU.pow)
+            if batches[bi]["masked"]:
+                nc.gpsimd.memset(ee[64:128, 0, n - 1:n], 0.0)
+
+        def sm_c(bi):
+            (nr, n) = dims(bi)
+            ee = small[(bi, "ee")]
+            sv = sm_tile(bi, "sv", 1)
+            nc.vector.tensor_reduce(out=sv[:, 0:nr, 0], in_=ee[:, 0:nr, 0:n], axis=AX.X, op=ALU.add)
+            rv = sm_tile(bi, "rv", 1)
+            nc.vector.reciprocal(out=rv[:, 0:nr, :], in_=sv[:, 0:nr, :])
+            aa = sm_tile(bi, "aa", NPOS)
+            nc.vector.tensor_tensor(out=aa[:, 0:nr, 0:n], in0=ee[:, 0:nr, 0:n],
+                                    in1=rv[:, 0:nr, :].to_broadcast([P, nr, n]), op=ALU.mult)
+            for rr in range(nr):
+                state["chains"].append([bi, rr, 0])
+
+        later_x = {6: 2, 8: 3}
+        for t in range(n_units + LAG_C + 1):
             if t < n_units:
                 stage1(t)
             if t in later_x:
                 s = later_x[t]
-                xprep_q(s, xprep_t(s))
-            if 0 <= t - 2 < n_units:
-                evac(t - 2)
+                xgl = xprep_t(s)
+            used = 0
             if 0 <= t - 1 < n_units:
-                regroup_quant(t - 1)
+                regroup(t - 1)
+            used += e3_steps(2)
+            if 0 <= t - 2 < n_units:
+                evac_alloc(t - 2)
+                evac(t - 2, 0)
+            if 0 <= t - 1 < n_units:
+                quant(t - 1)
                 stage2(t - 1)
-            for ri in range(len(rows)):
-                if last_unit[ri] == t - 2:
-                    sm_a(ri)
-                if last_unit[ri] == t - 3:
-                    sm_b(ri)
-                if last_unit[ri] == t - 4:
-                    sm_c(ri)
+            used += e3_steps(2)
+            if 0 <= t - 2 < n_units:
+                evac(t - 2, 1)
+            if t in later_x:
+                xprep_q(later_x[t], xgl)
+            if 0 <= t - 3 < n_units:
+                squares(t - 3)
+            for bi in range(len(batches)):
+                if batches[bi]["direct"]:
+                    continue
+                if last_unit[bi] == t - 3:
+                    sm_a(bi)
+                if last_unit[bi] == t - LAG_B:
+                    sm_b(bi)
+                if last_unit[bi] == t - LAG_C:
+                    sm_c(bi)
+            e3_steps(E3CAP - used)
+        while e3_step():
+            pass

@@ -23,7 +23,7 @@ LOG2E = 1.4426950408889634
 FLOPS = 2 * 11520 * 512 * 512 + 2 * 11520 * 512 * 256
 
 PBUFS = 17
-E3CAP = 6
+GAP = 2
 R_ON_SCALAR = ()
 PINNED = True
 LAG_B = 5
@@ -109,19 +109,21 @@ def tile_lpair_t_kernel(tc, x, W1, b1, W2, b2, out):
             s = keep.tile([P, width], U8, name=nm + "_s", align_bytes=64)
             return (c, s)
 
+        def half_codes(nm, full):
+            c = keep.tile([P, HID], U32, name=nm + "_c", align_bytes=64)
+            nc.vector.memset(c[:].bitcast(I32), 0)
+            return (c, full[1])
+
         w_e = code_tiles("w_e", HID)
         w_n = code_tiles("w_n", HID)
-        wi = [code_tiles("wi0", HID), code_tiles("wi1", HID)]
-        wj = [code_tiles("wj0", HID), code_tiles("wj1", HID)]
+        wi = [half_codes("wi0", w_n), half_codes("wi1", w_e)]
+        wj = [half_codes("wj0", w_e), half_codes("wj1", w_n)]
         w2q = code_tiles("w2q", D)
         xq = [code_tiles("xq%d" % s, HID) for s in range(4)]
         warm = keep.tile([P, 1], F32, name="warm")
         nc.vector.memset(warm[:], 0.0)
         junk = keep.tile([P, D], BF16, name="junk")
         nc.scalar.activation(out=junk[:, 0:1], in_=warm[:], func=ACT.Gelu)
-        for (c, s) in wi + wj:
-            nc.vector.memset(c[:].bitcast(I32), 0)
-            nc.vector.memset(s[:].bitcast(I32), 0)
         b1f = keep.tile([P, CH], F32, name="b1f")
         b2f = keep.tile([P, 2, D], F32, name="b2f")
         otile = [keep.tile([P, NPOS, D], F32, name="o0"), keep.tile([P, NPOS, D], F32, name="o1"),
@@ -152,25 +154,25 @@ def tile_lpair_t_kernel(tc, x, W1, b1, W2, b2, out):
             nc.vector.quantize_mx(out=full[0][:].bitcast(FP8X4), scales=full[1][:],
                                   in_=g[:].rearrange("p w j -> p (w j)"))
             for (dst, lo, hi) in ((top, 0, 64), (bottom, 64, 128)):
-                for t in range(2):
-                    nc.vector.tensor_copy(out=dst[t][lo:hi, :].bitcast(I32), in_=full[t][lo:hi, :].bitcast(I32))
+                nc.vector.tensor_copy(out=dst[0][lo:hi, :].bitcast(I32), in_=full[0][lo:hi, :].bitcast(I32))
 
         xg0 = xprep_t(0)
+        xg1 = xprep_t(1)
         g_s = w1_regroup(nc.vector.tensor_copy, w1raw_s)
-        g_n = w1_regroup(nc.scalar.copy, w1raw_n)
         nc.vector.tensor_copy(out=b1f[:], in_=b1b[:])
         w1_quant(g_s, w_e, wj[0], wi[1])
         xprep_q(0, xg0)
-        xg1 = xprep_t(1)
+        g_n = w1_regroup(nc.vector.tensor_copy, w1raw_n)
+        xprep_q(1, xg1)
         w1_quant(g_n, w_n, wi[0], wj[1])
         w2g = stage.tile([P, D, CH], BF16, name="w2g", align_bytes=64)
-        nc.vector.tensor_copy(out=w2g[:].rearrange("p (c i) t -> p c t i", i=4),
-                              in_=w2raw[:].rearrange("p t (c i) -> p c t i", i=4))
-        xprep_q(1, xg1)
+        nc.gpsimd.tensor_scalar(out=w2g[:].rearrange("p (c i) t -> p c t i", i=4),
+                                in0=w2raw[:].rearrange("p t (c i) -> p c t i", i=4),
+                                scalar1=1.0, scalar2=0.0, op0=ALU.mult, op1=ALU.add)
+        nc.gpsimd.tensor_scalar(out=b2f[:], in0=b2b[:].unsqueeze(1).to_broadcast([P, 2, D]),
+                                scalar1=1.0, scalar2=0.0, op0=ALU.mult, op1=ALU.add)
         nc.vector.quantize_mx(out=w2q[0][:].bitcast(FP8X4), scales=w2q[1][:],
                               in_=w2g[:].rearrange("p w j -> p (w j)"))
-        for h in range(2):
-            nc.vector.tensor_copy(out=b2f[:, h, :], in_=b2b[:])
 
         def mx(reg, w, c, src, blk, start, stop):
             cols = slice(c * P, (c + 1) * P)
@@ -186,7 +188,7 @@ def tile_lpair_t_kernel(tc, x, W1, b1, W2, b2, out):
         pts = {}
         small = {}
         left = {}
-        state = {"rr": 0, "chains": []}
+        state = {"last": None, "chains": []}
 
         def stage1(u):
             hp = hpool.tile([P, CH, UNIT * P], BF16, name="hp")
@@ -234,46 +236,66 @@ def tile_lpair_t_kernel(tc, x, W1, b1, W2, b2, out):
             small[(bi, nm)] = t
             return t
 
-        def e3_step():
-            chains = state["chains"]
+        def fill_one(force):
+            chains = [c for c in state["chains"] if len(c["ops"]) > c["at"]]
+            state["chains"] = chains
             if len(chains) == 0:
                 return False
-            state["rr"] = (state["rr"] + 1) % len(chains)
-            ch = chains[state["rr"]]
-            (bi, rr, idx) = (ch[0], ch[1], ch[2])
-            row = batches[bi]["rows"][rr]
-            aa = small[(bi, "aa")]
-            (u, k) = pos[(bi, rr, idx)]
-            acc = otile[row["g"]][:, row["orow"], :]
-            if idx == 0:
-                nc.vector.tensor_scalar(out=acc, in0=pts[u][:, k, :], scalar1=aa[:, rr, 0:1], scalar2=None,
-                                        op0=ALU.mult)
-            else:
-                nc.vector.scalar_tensor_tensor(out=acc, in0=pts[u][:, k, :], scalar=aa[:, rr, idx:idx + 1], in1=acc,
-                                               op0=ALU.mult, op1=ALU.add)
-            left[u] -= 1
-            ch[2] += 1
-            if ch[2] == len(row["js"]):
-                state["chains"] = [c for c in chains if c[2] < len(batches[c[0]]["rows"][c[1]]["js"])]
-                g = row["g"]
-                if g < 2:
-                    nc.sync.dma_start(out=out[g * P:(g + 1) * P, row["i"], :], in_=acc)
-                else:
-                    r = row["orow"]
-                    nc.sync.dma_start(out=out[2 * P:2 * P + 64, 2 * r + 1, :], in_=otile[2][0:64, r, :])
-                    nc.sync.dma_start(out=out[2 * P:2 * P + 64, 2 * r, :], in_=otile[2][64:128, r, :])
+            pick = None
+            for c in chains:
+                if c["key"] != state["last"]:
+                    pick = c
+                    break
+            if pick is None:
+                if not force:
+                    return False
+                pick = chains[0]
+            op = pick["ops"][pick["at"]]
+            pick["at"] += 1
+            state["last"] = pick["key"]
+            state["chains"] = [c for c in chains if c["key"] != pick["key"]] + [pick]
+            op()
             return True
 
-        def e3_steps(n):
+        def fill(n):
             done = 0
-            while done < n and e3_step():
+            while done < n and fill_one(False):
                 done += 1
             return done
+
+        def main_op():
+            state["last"] = None
+
+        def add_chain(key, ops):
+            state["chains"].append({"key": key, "ops": ops, "at": 0})
+
+        def e3_op(bi, rr, idx):
+            def emit():
+                row = batches[bi]["rows"][rr]
+                aa = small[(bi, "aa")]
+                (u, k) = pos[(bi, rr, idx)]
+                acc = otile[row["g"]][:, row["orow"], :]
+                if idx == 0:
+                    nc.vector.tensor_scalar(out=acc, in0=pts[u][:, k, :], scalar1=aa[:, rr, 0:1], scalar2=None,
+                                            op0=ALU.mult)
+                else:
+                    nc.vector.scalar_tensor_tensor(out=acc, in0=pts[u][:, k, :], scalar=aa[:, rr, idx:idx + 1],
+                                                   in1=acc, op0=ALU.mult, op1=ALU.add)
+                left[u] -= 1
+                if idx == len(row["js"]) - 1:
+                    g = row["g"]
+                    if g < 2:
+                        nc.sync.dma_start(out=out[g * P:(g + 1) * P, row["i"], :], in_=acc)
+                    else:
+                        r = row["orow"]
+                        nc.sync.dma_start(out=out[2 * P:2 * P + 64, 2 * r + 1, :], in_=otile[2][0:64, r, :])
+                        nc.sync.dma_start(out=out[2 * P:2 * P + 64, 2 * r, :], in_=otile[2][64:128, r, :])
+            return emit
 
         def evac_alloc(u):
             if u - PBUFS in left:
                 while left[u - PBUFS] > 0:
-                    assert e3_step()
+                    assert fill_one(True)
             pts[u] = ppool.tile([P, UNIT, D], F32, name="pt")
             left[u] = UNIT
 
@@ -308,61 +330,81 @@ def tile_lpair_t_kernel(tc, x, W1, b1, W2, b2, out):
             (nr, n) = dims(bi)
             nrm = small[(bi, "nrm")]
             mxv = sm_tile(bi, "mx", 1)
-            nc.vector.tensor_reduce(out=mxv[:, 0:nr, 0], in_=nrm[:, 0:nr, 0:n], axis=AX.X, op=ALU.max)
             dd = sm_tile(bi, "dd", NPOS)
-            nc.vector.tensor_tensor(out=dd[:, 0:nr, 0:n], in0=nrm[:, 0:nr, 0:n],
-                                    in1=mxv[:, 0:nr, :].to_broadcast([P, nr, n]), op=ALU.subtract)
             ee = sm_tile(bi, "ee", NPOS)
-            nc.gpsimd.tensor_tensor(out=ee[:, 0:nr, 0:n], in0=two[:, 0:nr, 0:n], in1=dd[:, 0:nr, 0:n], op=ALU.pow)
-            if batches[bi]["masked"]:
-                nc.gpsimd.memset(ee[64:128, 0, n - 1:n], 0.0)
+
+            def op_max():
+                nc.vector.tensor_reduce(out=mxv[:, 0:nr, 0], in_=nrm[:, 0:nr, 0:n], axis=AX.X, op=ALU.max)
+
+            def op_sub():
+                nc.vector.tensor_tensor(out=dd[:, 0:nr, 0:n], in0=nrm[:, 0:nr, 0:n],
+                                        in1=mxv[:, 0:nr, :].to_broadcast([P, nr, n]), op=ALU.subtract)
+                nc.gpsimd.tensor_tensor(out=ee[:, 0:nr, 0:n], in0=two[:, 0:nr, 0:n], in1=dd[:, 0:nr, 0:n],
+                                        op=ALU.pow)
+                if batches[bi]["masked"]:
+                    nc.gpsimd.memset(ee[64:128, 0, n - 1:n], 0.0)
+
+            add_chain(("b", bi), [op_max, op_sub])
 
         def sm_c(bi):
             (nr, n) = dims(bi)
             ee = small[(bi, "ee")]
             sv = sm_tile(bi, "sv", 1)
-            nc.vector.tensor_reduce(out=sv[:, 0:nr, 0], in_=ee[:, 0:nr, 0:n], axis=AX.X, op=ALU.add)
             rv = sm_tile(bi, "rv", 1)
-            nc.vector.reciprocal(out=rv[:, 0:nr, :], in_=sv[:, 0:nr, :])
             aa = sm_tile(bi, "aa", NPOS)
-            nc.vector.tensor_tensor(out=aa[:, 0:nr, 0:n], in0=ee[:, 0:nr, 0:n],
-                                    in1=rv[:, 0:nr, :].to_broadcast([P, nr, n]), op=ALU.mult)
-            for rr in range(nr):
-                state["chains"].append([bi, rr, 0])
+
+            def op_sum():
+                nc.vector.tensor_reduce(out=sv[:, 0:nr, 0], in_=ee[:, 0:nr, 0:n], axis=AX.X, op=ALU.add)
+
+            def op_rec():
+                nc.vector.reciprocal(out=rv[:, 0:nr, :], in_=sv[:, 0:nr, :])
+
+            def op_mul():
+                nc.vector.tensor_tensor(out=aa[:, 0:nr, 0:n], in0=ee[:, 0:nr, 0:n],
+                                        in1=rv[:, 0:nr, :].to_broadcast([P, nr, n]), op=ALU.mult)
+                for rr in range(nr):
+                    add_chain(("e", bi, rr), [e3_op(bi, rr, idx) for idx in range(n)])
+
+            add_chain(("c", bi), [op_sum, op_rec, op_mul])
 
         later_x = {6: 2, 8: 3}
         for t in range(n_units + LAG_C + 1):
             if t < n_units:
                 stage1(t)
             if t in later_x:
-                s = later_x[t]
-                xgl = xprep_t(s)
-            used = 0
-            if 0 <= t - 1 < n_units:
-                regroup(t - 1)
-            used += e3_steps(2)
-            if 0 <= t - 2 < n_units:
-                evac_alloc(t - 2)
-                evac(t - 2, 0)
-            if 0 <= t - 1 < n_units:
-                quant(t - 1)
-                stage2(t - 1)
-            used += e3_steps(2)
-            if 0 <= t - 2 < n_units:
-                evac(t - 2, 1)
-            if t in later_x:
-                xprep_q(later_x[t], xgl)
-            if 0 <= t - 3 < n_units:
-                squares(t - 3)
+                xgl = xprep_t(later_x[t])
             for bi in range(len(batches)):
                 if batches[bi]["direct"]:
                     continue
-                if last_unit[bi] == t - 3:
-                    sm_a(bi)
                 if last_unit[bi] == t - LAG_B:
                     sm_b(bi)
                 if last_unit[bi] == t - LAG_C:
                     sm_c(bi)
-            e3_steps(E3CAP - used)
-        while e3_step():
+            if 0 <= t - 1 < n_units:
+                regroup(t - 1)
+                main_op()
+            fill(GAP)
+            if 0 <= t - 2 < n_units:
+                evac_alloc(t - 2)
+                evac(t - 2, 0)
+                main_op()
+            fill(GAP)
+            if 0 <= t - 1 < n_units:
+                quant(t - 1)
+                main_op()
+                stage2(t - 1)
+            fill(GAP)
+            if 0 <= t - 2 < n_units:
+                evac(t - 2, 1)
+                main_op()
+            fill(GAP)
+            if t in later_x:
+                xprep_q(later_x[t], xgl)
+                main_op()
+            if 0 <= t - 3 < n_units:
+                squares(t - 3)
+            for bi in range(len(batches)):
+                if not batches[bi]["direct"] and last_unit[bi] == t - 3:
+                    sm_a(bi)
+        while fill_one(True):
             pass

@@ -22,7 +22,7 @@ UNIT = 4
 LOG2E = 1.4426950408889634
 FLOPS = 2 * 11520 * 512 * 512 + 2 * 11520 * 512 * 256
 
-PBUFS = 17
+PBUFS = 20
 GAP = 2
 R_ON_SCALAR = ()
 PINNED = True
@@ -30,32 +30,37 @@ LAG_B = 5
 LAG_C = 7
 
 
-def full_row(g, i):
-    js = list(range(0, i + 1, 2)) + list(range(1, i + 1, 2))
-    return {"g": g, "isrc": g, "jsrc": g, "i": i, "js": js, "orow": i}
-
-
 def build_batches():
     batches = []
-    for i in (7, 6, 5):
-        batches.append({"rows": [full_row(0, i), full_row(1, i)], "masked": False, "direct": False})
-    for r in (3, 2, 1, 0):
-        row = {"g": 2, "isrc": 3, "jsrc": 2, "i": 2 * r + 1, "js": list(range(2 * r + 2)), "orow": r}
+    for i in range(NPOS):
+        rows = [{"g": g, "isrc": g, "jsrc": g, "i": i, "js": list(range(i, -1, -1)), "orow": i} for g in range(2)]
+        batches.append({"rows": rows, "masked": False, "direct": i == 0})
+    for r in range(4):
+        row = {"g": 2, "isrc": 3, "jsrc": 2, "i": 2 * r + 1, "js": list(range(2 * r + 1, -1, -1)), "orow": r}
         batches.append({"rows": [row], "masked": True, "direct": False})
-    for i in (4, 3, 2, 1):
-        batches.append({"rows": [full_row(0, i), full_row(1, i)], "masked": False, "direct": False})
-    batches.append({"rows": [full_row(0, 0), full_row(1, 0)], "masked": False, "direct": True})
     return batches
+
+
+def build_slots():
+    slots = []
+    for d in (1, 0, 2, 3, 4, 5, 6, 7):
+        for g in range(2):
+            slots.extend([(i, g, d) for i in (3, 5, 7) if i >= d])
+    for d in range(NPOS):
+        slots.extend([(NPOS + r, 0, d) for r in range(4) if 2 * r + 1 >= d])
+    for d in range(NPOS - 1):
+        for g in range(2):
+            slots.extend([(i, g, d) for i in (4, 6) if i >= d])
+    for i in (2, 1, 0):
+        for g in range(2):
+            slots.extend([(i, g, d) for d in range(i + 1)])
+    return slots
 
 
 def tile_lpair_t_kernel(tc, x, W1, b1, W2, b2, out):
     nc = tc.nc
     batches = build_batches()
-    slots = []
-    for bi, bt in enumerate(batches):
-        for rr, row in enumerate(bt["rows"]):
-            for idx in range(len(row["js"])):
-                slots.append((bi, rr, idx))
+    slots = build_slots()
     n_units = len(slots) // UNIT
     assert n_units * UNIT == len(slots)
     units = [slots[u * UNIT:(u + 1) * UNIT] for u in range(n_units)]
@@ -174,12 +179,30 @@ def tile_lpair_t_kernel(tc, x, W1, b1, W2, b2, out):
         nc.vector.quantize_mx(out=w2q[0][:].bitcast(FP8X4), scales=w2q[1][:],
                               in_=w2g[:].rearrange("p w j -> p (w j)"))
 
-        def mx(reg, w, c, src, blk, start, stop):
+        def mx(reg, w, c, src, blk, nblk, start, stop):
             cols = slice(c * P, (c + 1) * P)
-            bc = slice(blk * P, (blk + 1) * P)
+            bc = slice(blk * P, (blk + nblk) * P)
             nc.tensor.matmul_mx(out=reg, lhsT=w[0][:, cols].bitcast(FP8X4), lhsT_scale=w[1][:, cols],
                                 rhs=xq[src][0][:, bc].bitcast(FP8X4), rhs_scale=xq[src][1][:, bc],
                                 start=start, stop=stop)
+
+        def slot_ij(s):
+            row = batches[s[0]]["rows"][s[1]]
+            return (row["isrc"], row["jsrc"], row["i"], row["js"][s[2]])
+
+        def pieces(u):
+            res = []
+            k = 0
+            while k < UNIT:
+                (si, sj, i, j) = slot_ij(units[u][k])
+                n = 1
+                while k + n < UNIT and slot_ij(units[u][k + n]) == (si, sj, i + 2 * n, j + 2 * n):
+                    n += 1
+                if n == 3:
+                    n = 2
+                res.append((k, n, si, sj, i, j))
+                k += n
+            return res
 
         hps = {}
         hgs = {}
@@ -195,16 +218,13 @@ def tile_lpair_t_kernel(tc, x, W1, b1, W2, b2, out):
             hps[u] = hp
             for c in range(CH):
                 z = zpool.tile([P, UNIT * P], F32, name="z", tag="z")
-                for k, (bi, rr, idx) in enumerate(units[u]):
-                    row = batches[bi]["rows"][rr]
-                    i = row["i"]
-                    j = row["js"][idx]
-                    reg = z[:, k * P:(k + 1) * P]
-                    if row["isrc"] == row["jsrc"] and i == j + 1 and j % 2 == 0:
-                        mx(reg, w_e, c, row["isrc"], j // 2, True, True)
+                for (k, n, si, sj, i, j) in pieces(u):
+                    reg = z[:, k * P:(k + n) * P]
+                    if si == sj and i == j + 1 and j % 2 == 0:
+                        mx(reg, w_e, c, si, j // 2, n, True, True)
                     else:
-                        mx(reg, wi[i % 2], c, row["isrc"], i // 2, True, False)
-                        mx(reg, wj[j % 2], c, row["jsrc"], j // 2, False, True)
+                        mx(reg, wi[i % 2], c, si, i // 2, n, True, False)
+                        mx(reg, wj[j % 2], c, sj, j // 2, n, False, True)
                 nc.scalar.activation(out=hp[:, c, :], in_=z[:], func=ACT.Gelu, bias=b1f[:, c:c + 1], scale=1.0)
 
         def regroup(u):
@@ -324,7 +344,7 @@ def tile_lpair_t_kernel(tc, x, W1, b1, W2, b2, out):
             nc.gpsimd.tensor_tensor(out=nrm[:, 0:nr, 0:n], in0=small[(bi, "n2")][:, 0:nr, 0:n],
                                     in1=half[:, 0:nr, 0:n], op=ALU.pow)
             if batches[bi]["masked"]:
-                nc.gpsimd.memset(nrm[64:128, 0, n - 1:n], 0.0)
+                nc.gpsimd.memset(nrm[64:128, 0, 0:1], 0.0)
 
         def sm_b(bi):
             (nr, n) = dims(bi)
@@ -342,7 +362,7 @@ def tile_lpair_t_kernel(tc, x, W1, b1, W2, b2, out):
                 nc.gpsimd.tensor_tensor(out=ee[:, 0:nr, 0:n], in0=two[:, 0:nr, 0:n], in1=dd[:, 0:nr, 0:n],
                                         op=ALU.pow)
                 if batches[bi]["masked"]:
-                    nc.gpsimd.memset(ee[64:128, 0, n - 1:n], 0.0)
+                    nc.gpsimd.memset(ee[64:128, 0, 0:1], 0.0)
 
             add_chain(("b", bi), [op_max, op_sub])
 

@@ -19,48 +19,43 @@ D = 256
 HID = 512
 CH = 4
 UNIT = 4
-LOG2E = 1.4426950408889634
 FLOPS = 2 * 11520 * 512 * 512 + 2 * 11520 * 512 * 256
 
-PBUFS = 20
+PBUFS = 17
 GAP = 2
 R_ON_SCALAR = ()
 PINNED = True
-LAG_B = 5
-LAG_C = 7
+LAG_B = 6
+LAG_T = 0
+LAG_C = 1
+
+
+def full_row(g, i):
+    js = list(range(0, i + 1, 2)) + list(range(1, i + 1, 2))
+    return {"g": g, "isrc": g, "jsrc": g, "i": i, "js": js, "orow": i}
 
 
 def build_batches():
     batches = []
-    for i in range(NPOS):
-        rows = [{"g": g, "isrc": g, "jsrc": g, "i": i, "js": list(range(i, -1, -1)), "orow": i} for g in range(2)]
-        batches.append({"rows": rows, "masked": False, "direct": i == 0})
-    for r in range(4):
-        row = {"g": 2, "isrc": 3, "jsrc": 2, "i": 2 * r + 1, "js": list(range(2 * r + 1, -1, -1)), "orow": r}
+    for i in (7, 6, 5):
+        batches.append({"rows": [full_row(0, i), full_row(1, i)], "masked": False, "direct": False})
+    for r in (3, 2, 1, 0):
+        row = {"g": 2, "isrc": 3, "jsrc": 2, "i": 2 * r + 1, "js": list(range(2 * r + 2)), "orow": r}
         batches.append({"rows": [row], "masked": True, "direct": False})
+    for i in (4, 3, 2, 1):
+        batches.append({"rows": [full_row(0, i), full_row(1, i)], "masked": False, "direct": False})
+    batches.append({"rows": [full_row(0, 0), full_row(1, 0)], "masked": False, "direct": True})
     return batches
-
-
-def build_slots():
-    slots = []
-    for d in (1, 0, 2, 3, 4, 5, 6, 7):
-        for g in range(2):
-            slots.extend([(i, g, d) for i in (3, 5, 7) if i >= d])
-    for d in range(NPOS):
-        slots.extend([(NPOS + r, 0, d) for r in range(4) if 2 * r + 1 >= d])
-    for d in range(NPOS - 1):
-        for g in range(2):
-            slots.extend([(i, g, d) for i in (4, 6) if i >= d])
-    for i in (2, 1, 0):
-        for g in range(2):
-            slots.extend([(i, g, d) for d in range(i + 1)])
-    return slots
 
 
 def tile_lpair_t_kernel(tc, x, W1, b1, W2, b2, out):
     nc = tc.nc
     batches = build_batches()
-    slots = build_slots()
+    slots = []
+    for bi, bt in enumerate(batches):
+        for rr, row in enumerate(bt["rows"]):
+            for idx in range(len(row["js"])):
+                slots.append((bi, rr, idx))
     n_units = len(slots) // UNIT
     assert n_units * UNIT == len(slots)
     units = [slots[u * UNIT:(u + 1) * UNIT] for u in range(n_units)]
@@ -105,9 +100,7 @@ def tile_lpair_t_kernel(tc, x, W1, b1, W2, b2, out):
         ident = keep.tile([P, P], F32, name="ident")
         make_identity(nc, ident[:])
         half = keep.tile([P, 2, NPOS], F32, name="half")
-        two = keep.tile([P, 2, NPOS], F32, name="two")
         nc.gpsimd.memset(half[:], 0.5)
-        nc.gpsimd.memset(two[:], 2.0)
 
         def code_tiles(nm, width):
             c = keep.tile([P, width], U32, name=nm + "_c", align_bytes=64)
@@ -127,6 +120,8 @@ def tile_lpair_t_kernel(tc, x, W1, b1, W2, b2, out):
         xq = [code_tiles("xq%d" % s, HID) for s in range(4)]
         warm = keep.tile([P, 1], F32, name="warm")
         nc.vector.memset(warm[:], 0.0)
+        one = keep.tile([P, 1], F32, name="one")
+        nc.vector.memset(one[:], 1.0)
         junk = keep.tile([P, D], BF16, name="junk")
         nc.scalar.activation(out=junk[:, 0:1], in_=warm[:], func=ACT.Gelu)
         b1f = keep.tile([P, CH], F32, name="b1f")
@@ -179,30 +174,12 @@ def tile_lpair_t_kernel(tc, x, W1, b1, W2, b2, out):
         nc.vector.quantize_mx(out=w2q[0][:].bitcast(FP8X4), scales=w2q[1][:],
                               in_=w2g[:].rearrange("p w j -> p (w j)"))
 
-        def mx(reg, w, c, src, blk, nblk, start, stop):
+        def mx(reg, w, c, src, blk, start, stop):
             cols = slice(c * P, (c + 1) * P)
-            bc = slice(blk * P, (blk + nblk) * P)
+            bc = slice(blk * P, (blk + 1) * P)
             nc.tensor.matmul_mx(out=reg, lhsT=w[0][:, cols].bitcast(FP8X4), lhsT_scale=w[1][:, cols],
                                 rhs=xq[src][0][:, bc].bitcast(FP8X4), rhs_scale=xq[src][1][:, bc],
                                 start=start, stop=stop)
-
-        def slot_ij(s):
-            row = batches[s[0]]["rows"][s[1]]
-            return (row["isrc"], row["jsrc"], row["i"], row["js"][s[2]])
-
-        def pieces(u):
-            res = []
-            k = 0
-            while k < UNIT:
-                (si, sj, i, j) = slot_ij(units[u][k])
-                n = 1
-                while k + n < UNIT and slot_ij(units[u][k + n]) == (si, sj, i + 2 * n, j + 2 * n):
-                    n += 1
-                if n == 3:
-                    n = 2
-                res.append((k, n, si, sj, i, j))
-                k += n
-            return res
 
         hps = {}
         hgs = {}
@@ -210,21 +187,25 @@ def tile_lpair_t_kernel(tc, x, W1, b1, W2, b2, out):
         qbs = {}
         pts = {}
         small = {}
+        tanh_at = {}
         left = {}
-        state = {"last": None, "chains": []}
+        state = {"last": None, "chains": [], "t": 0}
 
         def stage1(u):
             hp = hpool.tile([P, CH, UNIT * P], BF16, name="hp")
             hps[u] = hp
             for c in range(CH):
                 z = zpool.tile([P, UNIT * P], F32, name="z", tag="z")
-                for (k, n, si, sj, i, j) in pieces(u):
-                    reg = z[:, k * P:(k + n) * P]
-                    if si == sj and i == j + 1 and j % 2 == 0:
-                        mx(reg, w_e, c, si, j // 2, n, True, True)
+                for k, (bi, rr, idx) in enumerate(units[u]):
+                    row = batches[bi]["rows"][rr]
+                    i = row["i"]
+                    j = row["js"][idx]
+                    reg = z[:, k * P:(k + 1) * P]
+                    if row["isrc"] == row["jsrc"] and i == j + 1 and j % 2 == 0:
+                        mx(reg, w_e, c, row["isrc"], j // 2, True, True)
                     else:
-                        mx(reg, wi[i % 2], c, si, i // 2, n, True, False)
-                        mx(reg, wj[j % 2], c, sj, j // 2, n, False, True)
+                        mx(reg, wi[i % 2], c, row["isrc"], i // 2, True, False)
+                        mx(reg, wj[j % 2], c, row["jsrc"], j // 2, False, True)
                 nc.scalar.activation(out=hp[:, c, :], in_=z[:], func=ACT.Gelu, bias=b1f[:, c:c + 1], scale=1.0)
 
         def regroup(u):
@@ -332,7 +313,7 @@ def tile_lpair_t_kernel(tc, x, W1, b1, W2, b2, out):
                     continue
                 if (bi, "n2") not in small:
                     sm_tile(bi, "n2", NPOS)
-                nc.scalar.activation(out=junk[:], in_=pts[u][:, k, :], func=ACT.Square, scale=LOG2E,
+                nc.scalar.activation(out=junk[:], in_=pts[u][:, k, :], func=ACT.Square, scale=0.5,
                                      accum_out=small[(bi, "n2")][:, rr, idx:idx + 1])
 
         def dims(bi):
@@ -344,34 +325,53 @@ def tile_lpair_t_kernel(tc, x, W1, b1, W2, b2, out):
             nc.gpsimd.tensor_tensor(out=nrm[:, 0:nr, 0:n], in0=small[(bi, "n2")][:, 0:nr, 0:n],
                                     in1=half[:, 0:nr, 0:n], op=ALU.pow)
             if batches[bi]["masked"]:
-                nc.gpsimd.memset(nrm[64:128, 0, 0:1], 0.0)
+                nc.gpsimd.memset(nrm[64:128, 0, n - 1:n], 0.0)
 
         def sm_b(bi):
             (nr, n) = dims(bi)
             nrm = small[(bi, "nrm")]
             mxv = sm_tile(bi, "mx", 1)
-            dd = sm_tile(bi, "dd", NPOS)
-            ee = sm_tile(bi, "ee", NPOS)
 
             def op_max():
                 nc.vector.tensor_reduce(out=mxv[:, 0:nr, 0], in_=nrm[:, 0:nr, 0:n], axis=AX.X, op=ALU.max)
+                at = state["t"] + LAG_T
+                tanh_at[at] = tanh_at.get(at, []) + [bi]
 
-            def op_sub():
-                nc.vector.tensor_tensor(out=dd[:, 0:nr, 0:n], in0=nrm[:, 0:nr, 0:n],
-                                        in1=mxv[:, 0:nr, :].to_broadcast([P, nr, n]), op=ALU.subtract)
-                nc.gpsimd.tensor_tensor(out=ee[:, 0:nr, 0:n], in0=two[:, 0:nr, 0:n], in1=dd[:, 0:nr, 0:n],
-                                        op=ALU.pow)
-                if batches[bi]["masked"]:
-                    nc.gpsimd.memset(ee[64:128, 0, 0:1], 0.0)
+            add_chain(("b", bi), [op_max])
 
-            add_chain(("b", bi), [op_max, op_sub])
+        def sm_t(bi):
+            (nr, n) = dims(bi)
+            nrm = small[(bi, "nrm")]
+            mxv = small[(bi, "mx")]
+            th = sm_tile(bi, "th", NPOS)
+            uu = sm_tile(bi, "uu", NPOS)
+            vv = sm_tile(bi, "vv", NPOS)
+            for rr in range(nr):
+                nc.scalar.activation(out=th[:, rr, 0:n], in_=nrm[:, rr, 0:n], func=ACT.Tanh, bias=mxv[:, rr, 0:1],
+                                     scale=-1.0)
+            nc.scalar.activation(out=uu[:, 0:nr, 0:n], in_=th[:, 0:nr, 0:n], func=ACT.Identity, bias=one[:, 0:1],
+                                 scale=-1.0)
+            nc.scalar.activation(out=vv[:, 0:nr, 0:n], in_=th[:, 0:nr, 0:n], func=ACT.Identity, bias=one[:, 0:1],
+                                 scale=1.0)
 
         def sm_c(bi):
             (nr, n) = dims(bi)
-            ee = small[(bi, "ee")]
+            uu = small[(bi, "uu")]
+            vv = small[(bi, "vv")]
+            rd = sm_tile(bi, "rd", NPOS)
+            ee = sm_tile(bi, "ee", NPOS)
             sv = sm_tile(bi, "sv", 1)
             rv = sm_tile(bi, "rv", 1)
             aa = sm_tile(bi, "aa", NPOS)
+
+            def op_rd():
+                nc.vector.reciprocal(out=rd[:, 0:nr, 0:n], in_=vv[:, 0:nr, 0:n])
+
+            def op_ee():
+                nc.vector.tensor_tensor(out=ee[:, 0:nr, 0:n], in0=uu[:, 0:nr, 0:n], in1=rd[:, 0:nr, 0:n], op=ALU.mult)
+
+            def op_mask():
+                nc.vector.memset(ee[64:128, 0, n - 1:n], 0.0)
 
             def op_sum():
                 nc.vector.tensor_reduce(out=sv[:, 0:nr, 0], in_=ee[:, 0:nr, 0:n], axis=AX.X, op=ALU.add)
@@ -385,21 +385,23 @@ def tile_lpair_t_kernel(tc, x, W1, b1, W2, b2, out):
                 for rr in range(nr):
                     add_chain(("e", bi, rr), [e3_op(bi, rr, idx) for idx in range(n)])
 
-            add_chain(("c", bi), [op_sum, op_rec, op_mul])
+            ops = [op_rd, op_ee] + ([op_mask] if batches[bi]["masked"] else []) + [op_sum, op_rec, op_mul]
+            add_chain(("c", bi), ops)
 
         later_x = {6: 2, 8: 3}
-        for t in range(n_units + LAG_C + 1):
+        for t in range(n_units + 14):
+            state["t"] = t
             if t < n_units:
                 stage1(t)
             if t in later_x:
                 xgl = xprep_t(later_x[t])
+            for bi in tanh_at.get(t - LAG_C, []):
+                sm_c(bi)
             for bi in range(len(batches)):
                 if batches[bi]["direct"]:
                     continue
                 if last_unit[bi] == t - LAG_B:
                     sm_b(bi)
-                if last_unit[bi] == t - LAG_C:
-                    sm_c(bi)
             if 0 <= t - 1 < n_units:
                 regroup(t - 1)
                 main_op()
@@ -423,6 +425,8 @@ def tile_lpair_t_kernel(tc, x, W1, b1, W2, b2, out):
                 main_op()
             if 0 <= t - 3 < n_units:
                 squares(t - 3)
+            for bi in tanh_at.get(t, []):
+                sm_t(bi)
             for bi in range(len(batches)):
                 if not batches[bi]["direct"] and last_unit[bi] == t - 3:
                     sm_a(bi)

@@ -146,8 +146,8 @@ def tile_lpair_t_kernel(tc, x, W1, b1, W2, b2, out):
 
         def w1_regroup(eng_copy, raw):
             g = stage.tile([P, HID, CH], BF16, name="w1g", align_bytes=64)
-            eng_copy(out=g[:].rearrange("p (c m) j -> p c m j", c=CH),
-                     in_=raw[:].rearrange("p j (m c) -> p c m j", c=CH))
+            eng_copy(out=g[:].rearrange("p (c m) j -> p m c j", c=CH),
+                     in_=raw[:].rearrange("p j (m c) -> p m c j", c=CH))
             return g
 
         def w1_quant(g, full, top, bottom):

@@ -174,9 +174,9 @@ def tile_lpair_t_kernel(tc, x, W1, b1, W2, b2, out):
         nc.vector.quantize_mx(out=w2q[0][:].bitcast(FP8X4), scales=w2q[1][:],
                               in_=w2g[:].rearrange("p w j -> p (w j)"))
 
-        def mx(reg, w, c, src, blk, start, stop):
+        def mx(reg, w, c, src, blk, start, stop, nblk=1):
             cols = slice(c * P, (c + 1) * P)
-            bc = slice(blk * P, (blk + 1) * P)
+            bc = slice(blk * P, (blk + nblk) * P)
             nc.tensor.matmul_mx(out=reg, lhsT=w[0][:, cols].bitcast(FP8X4), lhsT_scale=w[1][:, cols],
                                 rhs=xq[src][0][:, bc].bitcast(FP8X4), rhs_scale=xq[src][1][:, bc],
                                 start=start, stop=stop)
@@ -191,21 +191,31 @@ def tile_lpair_t_kernel(tc, x, W1, b1, W2, b2, out):
         left = {}
         state = {"last": None, "chains": [], "t": 0}
 
+        def slot_ij(s):
+            row = batches[s[0]]["rows"][s[1]]
+            return (row["isrc"], row["jsrc"], row["i"], row["js"][s[2]])
+
         def stage1(u):
             hp = hpool.tile([P, CH, UNIT * P], BF16, name="hp")
             hps[u] = hp
             for c in range(CH):
                 z = zpool.tile([P, UNIT * P], F32, name="z", tag="z")
-                for k, (bi, rr, idx) in enumerate(units[u]):
-                    row = batches[bi]["rows"][rr]
-                    i = row["i"]
-                    j = row["js"][idx]
-                    reg = z[:, k * P:(k + 1) * P]
-                    if row["isrc"] == row["jsrc"] and i == j + 1 and j % 2 == 0:
-                        mx(reg, w_e, c, row["isrc"], j // 2, True, True)
+                k = 0
+                while k < UNIT:
+                    (si, sj, i, j) = slot_ij(units[u][k])
+                    n = 1
+                    while k + n < UNIT and slot_ij(units[u][k + n])[1] == sj and slot_ij(units[u][k + n])[3] == j + 2 * n:
+                        n += 1
+                    if n == 3:
+                        n = 2
+                    if n == 1 and si == sj and i == j + 1 and j % 2 == 0:
+                        mx(z[:, k * P:(k + 1) * P], w_e, c, si, j // 2, True, True)
                     else:
-                        mx(reg, wi[i % 2], c, row["isrc"], i // 2, True, False)
-                        mx(reg, wj[j % 2], c, row["jsrc"], j // 2, False, True)
+                        mx(z[:, k * P:(k + n) * P], wj[j % 2], c, sj, j // 2, True, False, n)
+                        for s in range(n):
+                            (si2, sj2, i2, j2) = slot_ij(units[u][k + s])
+                            mx(z[:, (k + s) * P:(k + s + 1) * P], wi[i2 % 2], c, si2, i2 // 2, False, s == n - 1)
+                    k += n
                 nc.scalar.activation(out=hp[:, c, :], in_=z[:], func=ACT.Gelu, bias=b1f[:, c:c + 1], scale=1.0)
 
         def regroup(u):

@@ -28,6 +28,7 @@ PINNED = True
 LAG_B = 6
 LAG_T = 0
 LAG_C = 1
+V_SQ = (3,)
 
 
 def full_row(g, i):
@@ -123,6 +124,7 @@ def tile_lpair_t_kernel(tc, x, W1, b1, W2, b2, out):
         one = keep.tile([P, 1], F32, name="one")
         nc.vector.memset(one[:], 1.0)
         junk = keep.tile([P, D], BF16, name="junk")
+        junk_v = keep.tile([P, D], BF16, name="junk_v")
         nc.scalar.activation(out=junk[:, 0:1], in_=warm[:], func=ACT.Gelu)
         b1f = keep.tile([P, CH], F32, name="b1f")
         b2f = keep.tile([P, 2, D], F32, name="b2f")
@@ -323,8 +325,14 @@ def tile_lpair_t_kernel(tc, x, W1, b1, W2, b2, out):
                     continue
                 if (bi, "n2") not in small:
                     sm_tile(bi, "n2", NPOS)
-                nc.scalar.activation(out=junk[:], in_=pts[u][:, k, :], func=ACT.Square, scale=0.5,
-                                     accum_out=small[(bi, "n2")][:, rr, idx:idx + 1])
+                if k in V_SQ:
+                    nc.vector.scalar_tensor_tensor(out=junk_v[:], in0=pts[u][:, k, :], scalar=0.25, in1=pts[u][:, k, :],
+                                                   op0=ALU.mult, op1=ALU.mult,
+                                                   accum_out=small[(bi, "n2")][:, rr, idx:idx + 1])
+                    main_op()
+                else:
+                    nc.scalar.activation(out=junk[:], in_=pts[u][:, k, :], func=ACT.Square, scale=0.5,
+                                         accum_out=small[(bi, "n2")][:, rr, idx:idx + 1])
 
         def dims(bi):
             return (len(batches[bi]["rows"]), len(batches[bi]["rows"][0]["js"]))

@@ -28,7 +28,9 @@ PINNED = True
 LAG_B = 6
 LAG_T = 0
 LAG_C = 1
-V_SQ = (3,)
+U_EARLY = 9
+V_SQ_EARLY = (3,)
+V_SQ_LATE = ()
 
 
 def full_row(g, i):
@@ -325,7 +327,7 @@ def tile_lpair_t_kernel(tc, x, W1, b1, W2, b2, out):
                     continue
                 if (bi, "n2") not in small:
                     sm_tile(bi, "n2", NPOS)
-                if k in V_SQ:
+                if k in (V_SQ_EARLY if u < U_EARLY else V_SQ_LATE):
                     nc.vector.scalar_tensor_tensor(out=junk_v[:], in0=pts[u][:, k, :], scalar=0.25, in1=pts[u][:, k, :],
                                                    op0=ALU.mult, op1=ALU.mult,
                                                    accum_out=small[(bi, "n2")][:, rr, idx:idx + 1])

@@ -30,7 +30,7 @@ LAG_T = 0
 LAG_C = 1
 U_EARLY = 9
 V_SQ_EARLY = (3,)
-V_SQ_LATE = ()
+V_SQ_LATE = (3,)
 
 
 def full_row(g, i):
@@ -327,7 +327,7 @@ def tile_lpair_t_kernel(tc, x, W1, b1, W2, b2, out):
                     continue
                 if (bi, "n2") not in small:
                     sm_tile(bi, "n2", NPOS)
-                if k in (V_SQ_EARLY if u < U_EARLY else V_SQ_LATE):
+                if k in (V_SQ_EARLY if u < U_EARLY else (V_SQ_LATE if u % 2 == 1 else ())):
                     nc.vector.scalar_tensor_tensor(out=junk_v[:], in0=pts[u][:, k, :], scalar=0.25, in1=pts[u][:, k, :],
                                                    op0=ALU.mult, op1=ALU.mult,
                                                    accum_out=small[(bi, "n2")][:, rr, idx:idx + 1])

@@ -364,19 +364,15 @@ def tile_lpair_t_kernel(tc, x, W1, b1, W2, b2, out):
             nrm = small[(bi, "nrm")]
             mxv = small[(bi, "mx")]
             th = sm_tile(bi, "th", NPOS)
-            uu = sm_tile(bi, "uu", NPOS)
             vv = sm_tile(bi, "vv", NPOS)
             for rr in range(nr):
                 nc.scalar.activation(out=th[:, rr, 0:n], in_=nrm[:, rr, 0:n], func=ACT.Tanh, bias=mxv[:, rr, 0:1],
                                      scale=-1.0)
-            nc.scalar.activation(out=uu[:, 0:nr, 0:n], in_=th[:, 0:nr, 0:n], func=ACT.Identity, bias=one[:, 0:1],
-                                 scale=-1.0)
             nc.scalar.activation(out=vv[:, 0:nr, 0:n], in_=th[:, 0:nr, 0:n], func=ACT.Identity, bias=one[:, 0:1],
                                  scale=1.0)
 
         def sm_c(bi):
             (nr, n) = dims(bi)
-            uu = small[(bi, "uu")]
             vv = small[(bi, "vv")]
             rd = sm_tile(bi, "rd", NPOS)
             ee = sm_tile(bi, "ee", NPOS)
@@ -388,7 +384,8 @@ def tile_lpair_t_kernel(tc, x, W1, b1, W2, b2, out):
                 nc.vector.reciprocal(out=rd[:, 0:nr, 0:n], in_=vv[:, 0:nr, 0:n])
 
             def op_ee():
-                nc.vector.tensor_tensor(out=ee[:, 0:nr, 0:n], in0=uu[:, 0:nr, 0:n], in1=rd[:, 0:nr, 0:n], op=ALU.mult)
+                nc.vector.tensor_scalar(out=ee[:, 0:nr, 0:n], in0=rd[:, 0:nr, 0:n], scalar1=2.0, scalar2=-1.0,
+                                        op0=ALU.mult, op1=ALU.add)
 
             def op_mask():
                 nc.vector.memset(ee[64:128, 0, n - 1:n], 0.0)
@@ -420,7 +417,7 @@ def tile_lpair_t_kernel(tc, x, W1, b1, W2, b2, out):
             for bi in range(len(batches)):
                 if batches[bi]["direct"]:
                     continue
-                if last_unit[bi] == t - LAG_B:
+                if last_unit[bi] == t - (LAG_B if bi < 8 else 4):
                     sm_b(bi)
             if 0 <= t - 1 < n_units:
                 regroup(t - 1)

@@ -71,7 +71,8 @@ def tile_lpair_t_kernel(tc, x, W1, b1, W2, b2, out):
 
     with ExitStack() as ctx:
         if PINNED:
-            ctx.enter_context(tc.manual_schedule())
+            ctx.enter_context(tc.manual_schedule(engines={mybir.EngineType.PE, mybir.EngineType.DVE,
+                                                          mybir.EngineType.Pool, mybir.EngineType.SP}))
         keep = ctx.enter_context(tc.tile_pool(name="keep", bufs=1))
         stage = ctx.enter_context(tc.tile_pool(name="stage", bufs=2))
         hpool = ctx.enter_context(tc.tile_pool(name="hpool", bufs=3))

@@ -71,8 +71,7 @@ def tile_lpair_t_kernel(tc, x, W1, b1, W2, b2, out):
 
     with ExitStack() as ctx:
         if PINNED:
-            ctx.enter_context(tc.manual_schedule(engines={mybir.EngineType.PE, mybir.EngineType.DVE,
-                                                          mybir.EngineType.Pool, mybir.EngineType.SP}))
+            ctx.enter_context(tc.manual_schedule(engines={mybir.EngineType.DVE}))
         keep = ctx.enter_context(tc.tile_pool(name="keep", bufs=1))
         stage = ctx.enter_context(tc.tile_pool(name="stage", bufs=2))
         hpool = ctx.enter_context(tc.tile_pool(name="hpool", bufs=3))
@@ -328,7 +327,7 @@ def tile_lpair_t_kernel(tc, x, W1, b1, W2, b2, out):
                     continue
                 if (bi, "n2") not in small:
                     sm_tile(bi, "n2", NPOS)
-                if k in (V_SQ_EARLY if u < U_EARLY else (V_SQ_LATE if u % 2 == 1 else ())):
+                if k in (V_SQ_EARLY if u < U_EARLY else ()):
                     nc.vector.scalar_tensor_tensor(out=junk_v[:], in0=pts[u][:, k, :], scalar=0.25, in1=pts[u][:, k, :],
                                                    op0=ALU.mult, op1=ALU.mult,
                                                    accum_out=small[(bi, "n2")][:, rr, idx:idx + 1])

@@ -23,7 +23,8 @@ FLOPS = 2 * 11520 * 512 * 512 + 2 * 11520 * 512 * 256
 
 PBUFS = 17
 GAP = 2
-R_ON_SCALAR = ()
+S_FROM = 12
+V_COLS = 352
 PINNED = True
 LAG_B = 6
 LAG_T = 0
@@ -81,7 +82,6 @@ def tile_lpair_t_kernel(tc, x, W1, b1, W2, b2, out):
 
         xs = [keep.tile([P, NPOS * D], BF16, name="xs%d" % s) for s in range(4)]
         w1raw_s = keep.tile([P, CH, HID], BF16, name="w1raw_s")
-        w1raw_n = keep.tile([P, CH, HID], BF16, name="w1raw_n")
         w2raw = keep.tile([P, CH, D], BF16, name="w2raw")
         b1b = keep.tile([P, CH], BF16, name="b1b")
         b2b = keep.tile([P, D], BF16, name="b2b")
@@ -89,7 +89,6 @@ def tile_lpair_t_kernel(tc, x, W1, b1, W2, b2, out):
         nc.sync.dma_start(out=w1raw_s[0:64], in_=W1[256:512, :].rearrange("(p j) w -> p j w", j=CH))
         nc.sync.dma_start(out=w1raw_s[64:128], in_=W1[0:256, :].rearrange("(p j) w -> p j w", j=CH))
         nc.sync.dma_start(out=b1b[:], in_=b1.rearrange("(m c) -> m c", c=CH))
-        nc.sync.dma_start(out=w1raw_n[:], in_=W1.rearrange("(p j) w -> p j w", j=CH))
         nc.sync.dma_start(out=xs[1][:], in_=x[P:2 * P].rearrange("b n d -> b (n d)"))
         nc.sync.dma_start(out=w2raw[:], in_=W2.rearrange("(p j) w -> p j w", j=CH))
         nc.sync.dma_start(out=b2b[:], in_=b2.partition_broadcast(P))
@@ -116,7 +115,8 @@ def tile_lpair_t_kernel(tc, x, W1, b1, W2, b2, out):
             return (c, full[1])
 
         w_e = code_tiles("w_e", HID)
-        w_n = code_tiles("w_n", HID)
+        w_n = (None, keep.tile([P, HID], U8, name="w_n_s", align_bytes=64))
+        nc.gpsimd.memset(w_e[1][:].bitcast(I32), 0)
         wi = [half_codes("wi0", w_n), half_codes("wi1", w_e)]
         wj = [half_codes("wj0", w_e), half_codes("wj1", w_n)]
         w2q = code_tiles("w2q", D)
@@ -142,7 +142,8 @@ def tile_lpair_t_kernel(tc, x, W1, b1, W2, b2, out):
                 for bb in range(2):
                     for e in range(2):
                         nc.tensor.transpose(xt[:, bb, e, :], xw[:, 2 * kb + bb, :, e], ident[:])
-                nc.scalar.copy(out=xgw[:, 2 * kb:2 * kb + 2, :, :], in_=xt[:].rearrange("p b e r -> p b r e"))
+                copy = nc.scalar.copy if s < 2 else nc.vector.tensor_copy
+                copy(out=xgw[:, 2 * kb:2 * kb + 2, :, :], in_=xt[:].rearrange("p b e r -> p b r e"))
             return xg
 
         def xprep_q(s, xg):
@@ -159,6 +160,10 @@ def tile_lpair_t_kernel(tc, x, W1, b1, W2, b2, out):
                                   in_=g[:].rearrange("p w j -> p (w j)"))
             for (dst, lo, hi) in ((top, 0, 64), (bottom, 64, 128)):
                 nc.vector.tensor_copy(out=dst[0][lo:hi, :].bitcast(I32), in_=full[0][lo:hi, :].bitcast(I32))
+            for (dst, lo) in ((wi[0][0], 0), (wj[1][0], 64)):
+                nc.sync.dma_start(out=dst[lo:lo + 64, :].bitcast(I32), in_=full[0][64 - lo:128 - lo, :].bitcast(I32))
+            for lo in (0, 64):
+                nc.sync.dma_start(out=w_n[1][lo:lo + 64, :].bitcast(I32), in_=full[1][64 - lo:128 - lo, :].bitcast(I32))
 
         xg0 = xprep_t(0)
         xg1 = xprep_t(1)
@@ -166,9 +171,7 @@ def tile_lpair_t_kernel(tc, x, W1, b1, W2, b2, out):
         nc.vector.tensor_copy(out=b1f[:], in_=b1b[:])
         w1_quant(g_s, w_e, wj[0], wi[1])
         xprep_q(0, xg0)
-        g_n = w1_regroup(nc.vector.tensor_copy, w1raw_n)
         xprep_q(1, xg1)
-        w1_quant(g_n, w_n, wi[0], wj[1])
         w2g = stage.tile([P, D, CH], BF16, name="w2g", align_bytes=64)
         nc.gpsimd.tensor_scalar(out=w2g[:].rearrange("p (c i) t -> p c t i", i=4),
                                 in0=w2raw[:].rearrange("p t (c i) -> p c t i", i=4),
@@ -177,6 +180,11 @@ def tile_lpair_t_kernel(tc, x, W1, b1, W2, b2, out):
                                 scalar1=1.0, scalar2=0.0, op0=ALU.mult, op1=ALU.add)
         nc.vector.quantize_mx(out=w2q[0][:].bitcast(FP8X4), scales=w2q[1][:],
                               in_=w2g[:].rearrange("p w j -> p (w j)"))
+
+        xg2 = xprep_t(2)
+        xg3 = xprep_t(3)
+        xprep_q(2, xg2)
+        xprep_q(3, xg3)
 
         def mx(reg, w, c, src, blk, start, stop, nblk=1):
             cols = slice(c * P, (c + 1) * P)
@@ -198,6 +206,9 @@ def tile_lpair_t_kernel(tc, x, W1, b1, W2, b2, out):
         def slot_ij(s):
             row = batches[s[0]]["rows"][s[1]]
             return (row["isrc"], row["jsrc"], row["i"], row["js"][s[2]])
+
+        def v_cols(u):
+            return V_COLS if u >= S_FROM else UNIT * P
 
         def stage1(u):
             hp = hpool.tile([P, CH, UNIT * P], BF16, name="hp")
@@ -221,12 +232,18 @@ def tile_lpair_t_kernel(tc, x, W1, b1, W2, b2, out):
                             mx(z[:, (k + s) * P:(k + s + 1) * P], wi[i2 % 2], c, si2, i2 // 2, False, s == n - 1)
                     k += n
                 nc.scalar.activation(out=hp[:, c, :], in_=z[:], func=ACT.Gelu, bias=b1f[:, c:c + 1], scale=1.0)
-
-        def regroup(u):
             hg = hpool.tile([P, UNIT * P, CH], BF16, name="hg", align_bytes=64)
             hgs[u] = hg
-            cp = nc.scalar.copy if u in R_ON_SCALAR else nc.vector.tensor_copy
-            cp(out=hg[:].rearrange("p (c i) t -> p c t i", i=4), in_=hps[u][:].rearrange("p t (c i) -> p c t i", i=4))
+            n = v_cols(u)
+            if n < UNIT * P:
+                nc.scalar.copy(out=hg[:, n:, :].rearrange("p (c i) t -> p c t i", i=4),
+                               in_=hps[u][:, :, n:].rearrange("p t (c i) -> p c t i", i=4))
+
+        def regroup(u):
+            n = v_cols(u)
+            hg = hgs[u]
+            nc.vector.tensor_copy(out=hg[:, 0:n, :].rearrange("p (c i) t -> p c t i", i=4),
+                                  in_=hps[u][:, :, 0:n].rearrange("p t (c i) -> p c t i", i=4))
 
         def quant(u):
             hc = hpool.tile([P, UNIT * P], U32, name="hc", align_bytes=64)
@@ -345,7 +362,7 @@ def tile_lpair_t_kernel(tc, x, W1, b1, W2, b2, out):
             nc.gpsimd.tensor_tensor(out=nrm[:, 0:nr, 0:n], in0=small[(bi, "n2")][:, 0:nr, 0:n],
                                     in1=half[:, 0:nr, 0:n], op=ALU.pow)
             if batches[bi]["masked"]:
-                nc.gpsimd.memset(nrm[64:128, 0, n - 1:n], 0.0)
+                nc.gpsimd.memset(nrm[64:128, 0, n - 1:n], -1e9)
 
         def sm_b(bi):
             (nr, n) = dims(bi)
@@ -387,9 +404,6 @@ def tile_lpair_t_kernel(tc, x, W1, b1, W2, b2, out):
                 nc.vector.tensor_scalar(out=ee[:, 0:nr, 0:n], in0=rd[:, 0:nr, 0:n], scalar1=2.0, scalar2=-1.0,
                                         op0=ALU.mult, op1=ALU.add)
 
-            def op_mask():
-                nc.vector.memset(ee[64:128, 0, n - 1:n], 0.0)
-
             def op_sum():
                 nc.vector.tensor_reduce(out=sv[:, 0:nr, 0], in_=ee[:, 0:nr, 0:n], axis=AX.X, op=ALU.add)
 
@@ -402,10 +416,10 @@ def tile_lpair_t_kernel(tc, x, W1, b1, W2, b2, out):
                 for rr in range(nr):
                     add_chain(("e", bi, rr), [e3_op(bi, rr, idx) for idx in range(n)])
 
-            ops = [op_rd, op_ee] + ([op_mask] if batches[bi]["masked"] else []) + [op_sum, op_rec, op_mul]
+            ops = [op_rd, op_ee, op_sum, op_rec, op_mul]
             add_chain(("c", bi), ops)
 
-        later_x = {6: 2, 8: 3}
+        later_x = {}
         for t in range(n_units + 14):
             state["t"] = t
             if t < n_units:
@@ -437,8 +451,8 @@ def tile_lpair_t_kernel(tc, x, W1, b1, W2, b2, out):
                 evac(t - 2, 1)
                 main_op()
             fill(GAP)
-            if t in later_x:
-                xprep_q(later_x[t], xgl)
+            if t - 1 in later_x:
+                xprep_q(later_x[t - 1], xgl)
                 main_op()
             if 0 <= t - 3 < n_units:
                 squares(t - 3)

@@ -23,13 +23,15 @@ FLOPS = 2 * 11520 * 512 * 512 + 2 * 11520 * 512 * 256
 
 PBUFS = 17
 GAP = 2
-S_FROM = 12
-V_COLS = 352
+G_ROWS = ((0, 0), (2, 0), (3, 0))
+G_RATE = 2
+S_FROM = 30
+V_COLS = 416
 PINNED = True
-LAG_B = 6
+LAG_B = 5
 LAG_T = 0
 LAG_C = 1
-U_EARLY = 9
+U_EARLY = 12
 V_SQ_EARLY = (3,)
 V_SQ_LATE = (3,)
 
@@ -41,14 +43,12 @@ def full_row(g, i):
 
 def build_batches():
     batches = []
-    for i in (7, 6, 5):
-        batches.append({"rows": [full_row(0, i), full_row(1, i)], "masked": False, "direct": False})
-    for r in (3, 2, 1, 0):
-        row = {"g": 2, "isrc": 3, "jsrc": 2, "i": 2 * r + 1, "js": list(range(2 * r + 2)), "orow": r}
-        batches.append({"rows": [row], "masked": True, "direct": False})
-    for i in (4, 3, 2, 1):
-        batches.append({"rows": [full_row(0, i), full_row(1, i)], "masked": False, "direct": False})
-    batches.append({"rows": [full_row(0, 0), full_row(1, 0)], "masked": False, "direct": True})
+    for kind, i in ((0, 7), (0, 3), (0, 5), (0, 6), (1, 3), (1, 2), (1, 1), (1, 0), (0, 4), (0, 2), (0, 1), (0, 0)):
+        if kind == 0:
+            batches.append({"rows": [full_row(0, i), full_row(1, i)], "masked": False, "direct": i == 0})
+        else:
+            row = {"g": 2, "isrc": 3, "jsrc": 2, "i": 2 * i + 1, "js": list(range(2 * i + 2)), "orow": i}
+            batches.append({"rows": [row], "masked": True, "direct": False})
     return batches
 
 
@@ -60,6 +60,8 @@ def tile_lpair_t_kernel(tc, x, W1, b1, W2, b2, out):
         for rr, row in enumerate(bt["rows"]):
             for idx in range(len(row["js"])):
                 slots.append((bi, rr, idx))
+        if bi == 0:
+            slots = sorted(slots, key=lambda s: batches[0]["rows"][s[1]]["js"][s[2]] % 2)
     n_units = len(slots) // UNIT
     assert n_units * UNIT == len(slots)
     units = [slots[u * UNIT:(u + 1) * UNIT] for u in range(n_units)]
@@ -77,6 +79,7 @@ def tile_lpair_t_kernel(tc, x, W1, b1, W2, b2, out):
         stage = ctx.enter_context(tc.tile_pool(name="stage", bufs=2))
         hpool = ctx.enter_context(tc.tile_pool(name="hpool", bufs=3))
         ppool = ctx.enter_context(tc.tile_pool(name="ppool", bufs=PBUFS))
+        gpool = ctx.enter_context(tc.tile_pool(name="gpool", bufs=2))
         zpool = ctx.enter_context(tc.psum_pool(name="zpool", bufs=5))
         qpool = ctx.enter_context(tc.psum_pool(name="qpool", bufs=3))
 
@@ -156,10 +159,12 @@ def tile_lpair_t_kernel(tc, x, W1, b1, W2, b2, out):
             return g
 
         def w1_quant(g, full, top, bottom):
-            nc.vector.quantize_mx(out=full[0][:].bitcast(FP8X4), scales=full[1][:],
-                                  in_=g[:].rearrange("p w j -> p (w j)"))
-            for (dst, lo, hi) in ((top, 0, 64), (bottom, 64, 128)):
-                nc.vector.tensor_copy(out=dst[0][lo:hi, :].bitcast(I32), in_=full[0][lo:hi, :].bitcast(I32))
+            for c in range(CH):
+                cols = slice(c * P, (c + 1) * P)
+                nc.vector.quantize_mx(out=full[0][:, cols].bitcast(FP8X4), scales=full[1][:, cols],
+                                      in_=g[:, cols, :].rearrange("p w j -> p (w j)"))
+                for (dst, lo, hi) in ((top, 0, 64), (bottom, 64, 128)):
+                    nc.vector.tensor_copy(out=dst[0][lo:hi, cols].bitcast(I32), in_=full[0][lo:hi, cols].bitcast(I32))
             for (dst, lo) in ((wi[0][0], 0), (wj[1][0], 64)):
                 nc.sync.dma_start(out=dst[lo:lo + 64, :].bitcast(I32), in_=full[0][64 - lo:128 - lo, :].bitcast(I32))
             for lo in (0, 64):
@@ -169,8 +174,8 @@ def tile_lpair_t_kernel(tc, x, W1, b1, W2, b2, out):
         xg1 = xprep_t(1)
         g_s = w1_regroup(nc.vector.tensor_copy, w1raw_s)
         nc.vector.tensor_copy(out=b1f[:], in_=b1b[:])
-        w1_quant(g_s, w_e, wj[0], wi[1])
         xprep_q(0, xg0)
+        w1_quant(g_s, w_e, wj[0], wi[1])
         xprep_q(1, xg1)
         w2g = stage.tile([P, D, CH], BF16, name="w2g", align_bytes=64)
         nc.gpsimd.tensor_scalar(out=w2g[:].rearrange("p (c i) t -> p c t i", i=4),
@@ -181,11 +186,6 @@ def tile_lpair_t_kernel(tc, x, W1, b1, W2, b2, out):
         nc.vector.quantize_mx(out=w2q[0][:].bitcast(FP8X4), scales=w2q[1][:],
                               in_=w2g[:].rearrange("p w j -> p (w j)"))
 
-        xg2 = xprep_t(2)
-        xg3 = xprep_t(3)
-        xprep_q(2, xg2)
-        xprep_q(3, xg3)
-
         def mx(reg, w, c, src, blk, start, stop, nblk=1):
             cols = slice(c * P, (c + 1) * P)
             bc = slice(blk * P, (blk + nblk) * P)
@@ -193,6 +193,7 @@ def tile_lpair_t_kernel(tc, x, W1, b1, W2, b2, out):
                                 rhs=xq[src][0][:, bc].bitcast(FP8X4), rhs_scale=xq[src][1][:, bc],
                                 start=start, stop=stop)
 
+        g_terms = []
         hps = {}
         hgs = {}
         hcs = {}
@@ -301,13 +302,26 @@ def tile_lpair_t_kernel(tc, x, W1, b1, W2, b2, out):
         def add_chain(key, ops):
             state["chains"].append({"key": key, "ops": ops, "at": 0})
 
-        def e3_op(bi, rr, idx):
+        def g_sum():
+            if len(g_terms) > 0:
+                e3_op(*g_terms.pop(0), True)()
+
+        def e3_op(bi, rr, idx, on_g=False):
             def emit():
                 row = batches[bi]["rows"][rr]
                 aa = small[(bi, "aa")]
                 (u, k) = pos[(bi, rr, idx)]
                 acc = otile[row["g"]][:, row["orow"], :]
-                if idx == 0:
+                if on_g:
+                    dst = acc
+                    if idx > 0:
+                        gt = gpool.tile([P, D], F32, name="gt")
+                        dst = gt[:]
+                    nc.gpsimd.tensor_scalar(out=dst, in0=pts[u][:, k, :], scalar1=aa[:, rr, idx:idx + 1], scalar2=0.0,
+                                            op0=ALU.mult, op1=ALU.add)
+                    if idx > 0:
+                        nc.gpsimd.tensor_tensor(out=acc, in0=acc, in1=dst, op=ALU.add)
+                elif idx == 0:
                     nc.vector.tensor_scalar(out=acc, in0=pts[u][:, k, :], scalar1=aa[:, rr, 0:1], scalar2=None,
                                             op0=ALU.mult)
                 else:
@@ -327,7 +341,9 @@ def tile_lpair_t_kernel(tc, x, W1, b1, W2, b2, out):
         def evac_alloc(u):
             if u - PBUFS in left:
                 while left[u - PBUFS] > 0:
-                    assert fill_one(True)
+                    if not fill_one(True):
+                        assert len(g_terms) > 0
+                        g_sum()
             pts[u] = ppool.tile([P, UNIT, D], F32, name="pt")
             left[u] = UNIT
 
@@ -414,18 +430,20 @@ def tile_lpair_t_kernel(tc, x, W1, b1, W2, b2, out):
                 nc.vector.tensor_tensor(out=aa[:, 0:nr, 0:n], in0=ee[:, 0:nr, 0:n],
                                         in1=rv[:, 0:nr, :].to_broadcast([P, nr, n]), op=ALU.mult)
                 for rr in range(nr):
-                    add_chain(("e", bi, rr), [e3_op(bi, rr, idx) for idx in range(n)])
+                    if (bi, rr) in G_ROWS:
+                        for idx in range(n):
+                            g_terms.append((bi, rr, idx))
+                    else:
+                        add_chain(("e", bi, rr), [e3_op(bi, rr, idx) for idx in range(n)])
 
             ops = [op_rd, op_ee, op_sum, op_rec, op_mul]
             add_chain(("c", bi), ops)
 
-        later_x = {}
+        later_x = {0: 2, 1: 3}
         for t in range(n_units + 14):
             state["t"] = t
             if t < n_units:
                 stage1(t)
-            if t in later_x:
-                xgl = xprep_t(later_x[t])
             for bi in tanh_at.get(t - LAG_C, []):
                 sm_c(bi)
             for bi in range(len(batches)):
@@ -454,6 +472,9 @@ def tile_lpair_t_kernel(tc, x, W1, b1, W2, b2, out):
             if t - 1 in later_x:
                 xprep_q(later_x[t - 1], xgl)
                 main_op()
+            if t in later_x:
+                xgl = xprep_t(later_x[t])
+                main_op()
             if 0 <= t - 3 < n_units:
                 squares(t - 3)
             for bi in tanh_at.get(t, []):
@@ -461,5 +482,9 @@ def tile_lpair_t_kernel(tc, x, W1, b1, W2, b2, out):
             for bi in range(len(batches)):
                 if not batches[bi]["direct"] and last_unit[bi] == t - 3:
                     sm_a(bi)
+            for q in range(G_RATE):
+                g_sum()
+        while len(g_terms) > 0:
+            g_sum()
         while fill_one(True):
             pass

@@ -23,15 +23,15 @@ FLOPS = 2 * 11520 * 512 * 512 + 2 * 11520 * 512 * 256
 
 PBUFS = 17
 GAP = 2
-G_ROWS = ((0, 0), (2, 0), (3, 0))
-G_RATE = 2
+FIRST_ON_S = 4
+FIRST_TO = 20
 S_FROM = 30
 V_COLS = 416
 PINNED = True
 LAG_B = 5
 LAG_T = 0
 LAG_C = 1
-U_EARLY = 12
+U_EARLY = 5
 V_SQ_EARLY = (3,)
 V_SQ_LATE = (3,)
 
@@ -79,7 +79,6 @@ def tile_lpair_t_kernel(tc, x, W1, b1, W2, b2, out):
         stage = ctx.enter_context(tc.tile_pool(name="stage", bufs=2))
         hpool = ctx.enter_context(tc.tile_pool(name="hpool", bufs=3))
         ppool = ctx.enter_context(tc.tile_pool(name="ppool", bufs=PBUFS))
-        gpool = ctx.enter_context(tc.tile_pool(name="gpool", bufs=2))
         zpool = ctx.enter_context(tc.psum_pool(name="zpool", bufs=5))
         qpool = ctx.enter_context(tc.psum_pool(name="qpool", bufs=3))
 
@@ -193,7 +192,6 @@ def tile_lpair_t_kernel(tc, x, W1, b1, W2, b2, out):
                                 rhs=xq[src][0][:, bc].bitcast(FP8X4), rhs_scale=xq[src][1][:, bc],
                                 start=start, stop=stop)
 
-        g_terms = []
         hps = {}
         hgs = {}
         hcs = {}
@@ -302,26 +300,13 @@ def tile_lpair_t_kernel(tc, x, W1, b1, W2, b2, out):
         def add_chain(key, ops):
             state["chains"].append({"key": key, "ops": ops, "at": 0})
 
-        def g_sum():
-            if len(g_terms) > 0:
-                e3_op(*g_terms.pop(0), True)()
-
-        def e3_op(bi, rr, idx, on_g=False):
+        def e3_op(bi, rr, idx):
             def emit():
                 row = batches[bi]["rows"][rr]
                 aa = small[(bi, "aa")]
                 (u, k) = pos[(bi, rr, idx)]
                 acc = otile[row["g"]][:, row["orow"], :]
-                if on_g:
-                    dst = acc
-                    if idx > 0:
-                        gt = gpool.tile([P, D], F32, name="gt")
-                        dst = gt[:]
-                    nc.gpsimd.tensor_scalar(out=dst, in0=pts[u][:, k, :], scalar1=aa[:, rr, idx:idx + 1], scalar2=0.0,
-                                            op0=ALU.mult, op1=ALU.add)
-                    if idx > 0:
-                        nc.gpsimd.tensor_tensor(out=acc, in0=acc, in1=dst, op=ALU.add)
-                elif idx == 0:
+                if idx == 0:
                     nc.vector.tensor_scalar(out=acc, in0=pts[u][:, k, :], scalar1=aa[:, rr, 0:1], scalar2=None,
                                             op0=ALU.mult)
                 else:
@@ -341,9 +326,7 @@ def tile_lpair_t_kernel(tc, x, W1, b1, W2, b2, out):
         def evac_alloc(u):
             if u - PBUFS in left:
                 while left[u - PBUFS] > 0:
-                    if not fill_one(True):
-                        assert len(g_terms) > 0
-                        g_sum()
+                    assert fill_one(True)
             pts[u] = ppool.tile([P, UNIT, D], F32, name="pt")
             left[u] = UNIT
 
@@ -429,12 +412,17 @@ def tile_lpair_t_kernel(tc, x, W1, b1, W2, b2, out):
             def op_mul():
                 nc.vector.tensor_tensor(out=aa[:, 0:nr, 0:n], in0=ee[:, 0:nr, 0:n],
                                         in1=rv[:, 0:nr, :].to_broadcast([P, nr, n]), op=ALU.mult)
+                first = 0
+                if FIRST_ON_S <= bi < FIRST_TO:
+                    first = 1
+                    for rr in range(nr):
+                        row = batches[bi]["rows"][rr]
+                        (u, k) = pos[(bi, rr, 0)]
+                        nc.scalar.activation(out=otile[row["g"]][:, row["orow"], :], in_=pts[u][:, k, :], func=ACT.Copy,
+                                             scale=aa[:, rr, 0:1])
+                        left[u] -= 1
                 for rr in range(nr):
-                    if (bi, rr) in G_ROWS:
-                        for idx in range(n):
-                            g_terms.append((bi, rr, idx))
-                    else:
-                        add_chain(("e", bi, rr), [e3_op(bi, rr, idx) for idx in range(n)])
+                    add_chain(("e", bi, rr), [e3_op(bi, rr, idx) for idx in range(first, n)])
 
             ops = [op_rd, op_ee, op_sum, op_rec, op_mul]
             add_chain(("c", bi), ops)
@@ -482,9 +470,5 @@ def tile_lpair_t_kernel(tc, x, W1, b1, W2, b2, out):
             for bi in range(len(batches)):
                 if not batches[bi]["direct"] and last_unit[bi] == t - 3:
                     sm_a(bi)
-            for q in range(G_RATE):
-                g_sum()
-        while len(g_terms) > 0:
-            g_sum()
         while fill_one(True):
             pass

@@ -25,6 +25,7 @@ PBUFS = 17
 GAP = 2
 FIRST_ON_S = 4
 FIRST_TO = 20
+SOFT_FIRST = 24
 S_FROM = 30
 V_COLS = 416
 PINNED = True
@@ -177,11 +178,9 @@ def tile_lpair_t_kernel(tc, x, W1, b1, W2, b2, out):
         w1_quant(g_s, w_e, wj[0], wi[1])
         xprep_q(1, xg1)
         w2g = stage.tile([P, D, CH], BF16, name="w2g", align_bytes=64)
-        nc.gpsimd.tensor_scalar(out=w2g[:].rearrange("p (c i) t -> p c t i", i=4),
-                                in0=w2raw[:].rearrange("p t (c i) -> p c t i", i=4),
-                                scalar1=1.0, scalar2=0.0, op0=ALU.mult, op1=ALU.add)
-        nc.gpsimd.tensor_scalar(out=b2f[:], in0=b2b[:].unsqueeze(1).to_broadcast([P, 2, D]),
-                                scalar1=1.0, scalar2=0.0, op0=ALU.mult, op1=ALU.add)
+        nc.vector.tensor_copy(out=w2g[:].rearrange("p (c i) t -> p c t i", i=4),
+                              in_=w2raw[:].rearrange("p t (c i) -> p c t i", i=4))
+        nc.vector.tensor_copy(out=b2f[:], in_=b2b[:].unsqueeze(1).to_broadcast([P, 2, D]))
         nc.vector.quantize_mx(out=w2q[0][:].bitcast(FP8X4), scales=w2q[1][:],
                               in_=w2g[:].rearrange("p w j -> p (w j)"))
 
@@ -273,7 +272,7 @@ def tile_lpair_t_kernel(tc, x, W1, b1, W2, b2, out):
             if len(chains) == 0:
                 return False
             pick = None
-            for c in chains:
+            for c in sorted(chains, key=lambda c: c["key"][0] == "e") if state["t"] >= SOFT_FIRST else chains:
                 if c["key"] != state["last"]:
                     pick = c
                     break

from contextlib import ExitStack

import concourse.mybir as mybir
from concourse.masks import make_identity

F32 = mybir.dt.float32
BF16 = mybir.dt.bfloat16
U32 = mybir.dt.uint32
U8 = mybir.dt.uint8
I32 = mybir.dt.int32
FP8X4 = mybir.dt.float8_e4m3fn_x4
ALU = mybir.AluOpType
ACT = mybir.ActivationFunctionType
AX = mybir.AxisListType

P = 128
NPOS = 8
D = 256
HID = 512
CH = 4
UNIT = 4
FLOPS = 2 * 11520 * 512 * 512 + 2 * 11520 * 512 * 256

PBUFS = 17
GAP = 2
FIRST_ON_S = 4
FIRST_TO = 20
SOFT_FIRST = 24
S_FROM = 30
V_COLS = 416
PINNED = True
LAG_B = 5
LAG_T = 0
LAG_C = 1
U_EARLY = 5
V_SQ_EARLY = (3,)
V_SQ_LATE = (3,)


def full_row(g, i):
    js = list(range(0, i + 1, 2)) + list(range(1, i + 1, 2))
    return {"g": g, "isrc": g, "jsrc": g, "i": i, "js": js, "orow": i}


def build_batches():
    batches = []
    for kind, i in ((0, 7), (0, 3), (0, 5), (0, 6), (1, 3), (1, 2), (1, 1), (1, 0), (0, 4), (0, 2), (0, 1), (0, 0)):
        if kind == 0:
            batches.append({"rows": [full_row(0, i), full_row(1, i)], "masked": False, "direct": i == 0})
        else:
            row = {"g": 2, "isrc": 3, "jsrc": 2, "i": 2 * i + 1, "js": list(range(2 * i + 2)), "orow": i}
            batches.append({"rows": [row], "masked": True, "direct": False})
    return batches


def tile_lpair_t_kernel(tc, x, W1, b1, W2, b2, out):
    nc = tc.nc
    batches = build_batches()
    slots = []
    for bi, bt in enumerate(batches):
        for rr, row in enumerate(bt["rows"]):
            for idx in range(len(row["js"])):
                slots.append((bi, rr, idx))
        if bi == 0:
            slots = sorted(slots, key=lambda s: batches[0]["rows"][s[1]]["js"][s[2]] % 2)
    n_units = len(slots) // UNIT
    assert n_units * UNIT == len(slots)
    units = [slots[u * UNIT:(u + 1) * UNIT] for u in range(n_units)]
    last_unit = {}
    pos = {}
    for u in range(n_units):
        for k, s in enumerate(units[u]):
            last_unit[s[0]] = u
            pos[s] = (u, k)

    with ExitStack() as ctx:
        if PINNED:
            ctx.enter_context(tc.manual_schedule(engines={mybir.EngineType.DVE}))
        keep = ctx.enter_context(tc.tile_pool(name="keep", bufs=1))
        stage = ctx.enter_context(tc.tile_pool(name="stage", bufs=2))
        hpool = ctx.enter_context(tc.tile_pool(name="hpool", bufs=3))
        ppool = ctx.enter_context(tc.tile_pool(name="ppool", bufs=PBUFS))
        zpool = ctx.enter_context(tc.psum_pool(name="zpool", bufs=5))
        qpool = ctx.enter_context(tc.psum_pool(name="qpool", bufs=3))

        xs = [keep.tile([P, NPOS * D], BF16, name="xs%d" % s) for s in range(4)]
        w1raw_s = keep.tile([P, CH, HID], BF16, name="w1raw_s")
        w2raw = keep.tile([P, CH, D], BF16, name="w2raw")
        b1b = keep.tile([P, CH], BF16, name="b1b")
        b2b = keep.tile([P, D], BF16, name="b2b")
        nc.sync.dma_start(out=xs[0][:], in_=x[0:P].rearrange("b n d -> b (n d)"))
        nc.sync.dma_start(out=w1raw_s[0:64], in_=W1[256:512, :].rearrange("(p j) w -> p j w", j=CH))
        nc.sync.dma_start(out=w1raw_s[64:128], in_=W1[0:256, :].rearrange("(p j) w -> p j w", j=CH))
        nc.sync.dma_start(out=b1b[:], in_=b1.rearrange("(m c) -> m c", c=CH))
        nc.sync.dma_start(out=xs[1][:], in_=x[P:2 * P].rearrange("b n d -> b (n d)"))
        nc.sync.dma_start(out=w2raw[:], in_=W2.rearrange("(p j) w -> p j w", j=CH))
        nc.sync.dma_start(out=b2b[:], in_=b2.partition_broadcast(P))
        tail = x[2 * P:2 * P + 64]
        nc.sync.dma_start(out=xs[2][0:64, :], in_=tail.rearrange("b n d -> b (n d)"))
        nc.sync.dma_start(out=xs[2][64:128, :], in_=tail.rearrange("b n d -> b (n d)"))
        nc.sync.dma_start(out=xs[3][0:64, :], in_=tail.rearrange("b n d -> b (n d)"))
        nc.sync.dma_start(out=xs[3][64:128, D:NPOS * D], in_=tail[:, 0:NPOS - 1, :].rearrange("b n d -> b (n d)"))
        nc.sync.dma_start(out=xs[3][64:128, 0:D], in_=tail[:, 0, :])

        ident = keep.tile([P, P], F32, name="ident")
        make_identity(nc, ident[:])
        half = keep.tile([P, 2, NPOS], F32, name="half")
        nc.gpsimd.memset(half[:], 0.5)

        def code_tiles(nm, width):
            c = keep.tile([P, width], U32, name=nm + "_c", align_bytes=64)
            s = keep.tile([P, width], U8, name=nm + "_s", align_bytes=64)
            return (c, s)

        def half_codes(nm, full):
            c = keep.tile([P, HID], U32, name=nm + "_c", align_bytes=64)
            nc.vector.memset(c[:].bitcast(I32), 0)
            return (c, full[1])

        w_e = code_tiles("w_e", HID)
        w_n = (None, keep.tile([P, HID], U8, name="w_n_s", align_bytes=64))
        nc.gpsimd.memset(w_e[1][:].bitcast(I32), 0)
        wi = [half_codes("wi0", w_n), half_codes("wi1", w_e)]
        wj = [half_codes("wj0", w_e), half_codes("wj1", w_n)]
        w2q = code_tiles("w2q", D)
        xq = [code_tiles("xq%d" % s, HID) for s in range(4)]
        warm = keep.tile([P, 1], F32, name="warm")
        nc.vector.memset(warm[:], 0.0)
        one = keep.tile([P, 1], F32, name="one")
        nc.vector.memset(one[:], 1.0)
        junk = keep.tile([P, D], BF16, name="junk")
        junk_v = keep.tile([P, D], BF16, name="junk_v")
        nc.scalar.activation(out=junk[:, 0:1], in_=warm[:], func=ACT.Gelu)
        b1f = keep.tile([P, CH], F32, name="b1f")
        b2f = keep.tile([P, 2, D], F32, name="b2f")
        otile = [keep.tile([P, NPOS, D], F32, name="o0"), keep.tile([P, NPOS, D], F32, name="o1"),
                 keep.tile([P, 4, D], F32, name="o2")]

        def xprep_t(s):
            xw = xs[s][:].bitcast(F32).rearrange("p (m q e) -> p m q e", m=4, e=2)
            xg = stage.tile([P, 4 * P * CH], BF16, name="xg", align_bytes=64)
            xgw = xg[:].bitcast(F32).rearrange("p (m r e) -> p m r e", m=4, e=2)
            for kb in range(2):
                xt = zpool.tile([P, 2, 2, P], F32, name="xt", tag="z")
                for bb in range(2):
                    for e in range(2):
                        nc.tensor.transpose(xt[:, bb, e, :], xw[:, 2 * kb + bb, :, e], ident[:])
                copy = nc.scalar.copy if s < 2 else nc.vector.tensor_copy
                copy(out=xgw[:, 2 * kb:2 * kb + 2, :, :], in_=xt[:].rearrange("p b e r -> p b r e"))
            return xg

        def xprep_q(s, xg):
            nc.vector.quantize_mx(out=xq[s][0][:].bitcast(FP8X4), scales=xq[s][1][:], in_=xg[:])

        def w1_regroup(eng_copy, raw):
            g = stage.tile([P, HID, CH], BF16, name="w1g", align_bytes=64)
            eng_copy(out=g[:].rearrange("p (c m) j -> p m c j", c=CH),
                     in_=raw[:].rearrange("p j (m c) -> p m c j", c=CH))
            return g

        def w1_quant(g, full, top, bottom):
            for c in range(CH):
                cols = slice(c * P, (c + 1) * P)
                nc.vector.quantize_mx(out=full[0][:, cols].bitcast(FP8X4), scales=full[1][:, cols],
                                      in_=g[:, cols, :].rearrange("p w j -> p (w j)"))
                for (dst, lo, hi) in ((top, 0, 64), (bottom, 64, 128)):
                    nc.vector.tensor_copy(out=dst[0][lo:hi, cols].bitcast(I32), in_=full[0][lo:hi, cols].bitcast(I32))
            for (dst, lo) in ((wi[0][0], 0), (wj[1][0], 64)):
                nc.sync.dma_start(out=dst[lo:lo + 64, :].bitcast(I32), in_=full[0][64 - lo:128 - lo, :].bitcast(I32))
            for lo in (0, 64):
                nc.sync.dma_start(out=w_n[1][lo:lo + 64, :].bitcast(I32), in_=full[1][64 - lo:128 - lo, :].bitcast(I32))

        xg0 = xprep_t(0)
        xg1 = xprep_t(1)
        g_s = w1_regroup(nc.vector.tensor_copy, w1raw_s)
        nc.vector.tensor_copy(out=b1f[:], in_=b1b[:])
        xprep_q(0, xg0)
        w1_quant(g_s, w_e, wj[0], wi[1])
        xprep_q(1, xg1)
        w2g = stage.tile([P, D, CH], BF16, name="w2g", align_bytes=64)
        nc.vector.tensor_copy(out=w2g[:].rearrange("p (c i) t -> p c t i", i=4),
                              in_=w2raw[:].rearrange("p t (c i) -> p c t i", i=4))
        nc.vector.tensor_copy(out=b2f[:], in_=b2b[:].unsqueeze(1).to_broadcast([P, 2, D]))
        nc.vector.quantize_mx(out=w2q[0][:].bitcast(FP8X4), scales=w2q[1][:],
                              in_=w2g[:].rearrange("p w j -> p (w j)"))

        def mx(reg, w, c, src, blk, start, stop, nblk=1):
            cols = slice(c * P, (c + 1) * P)
            bc = slice(blk * P, (blk + nblk) * P)
            nc.tensor.matmul_mx(out=reg, lhsT=w[0][:, cols].bitcast(FP8X4), lhsT_scale=w[1][:, cols],
                                rhs=xq[src][0][:, bc].bitcast(FP8X4), rhs_scale=xq[src][1][:, bc],
                                start=start, stop=stop)

        hps = {}
        hgs = {}
        hcs = {}
        qbs = {}
        pts = {}
        small = {}
        tanh_at = {}
        left = {}
        state = {"last": None, "chains": [], "t": 0}

        def slot_ij(s):
            row = batches[s[0]]["rows"][s[1]]
            return (row["isrc"], row["jsrc"], row["i"], row["js"][s[2]])

        def v_cols(u):
            return V_COLS if u >= S_FROM else UNIT * P

        def stage1(u):
            hp = hpool.tile([P, CH, UNIT * P], BF16, name="hp")
            hps[u] = hp
            for c in range(CH):
                z = zpool.tile([P, UNIT * P], F32, name="z", tag="z")
                k = 0
                while k < UNIT:
                    (si, sj, i, j) = slot_ij(units[u][k])
                    n = 1
                    while k + n < UNIT and slot_ij(units[u][k + n])[1] == sj and slot_ij(units[u][k + n])[3] == j + 2 * n:
                        n += 1
                    if n == 3:
                        n = 2
                    if n == 1 and si == sj and i == j + 1 and j % 2 == 0:
                        mx(z[:, k * P:(k + 1) * P], w_e, c, si, j // 2, True, True)
                    else:
                        mx(z[:, k * P:(k + n) * P], wj[j % 2], c, sj, j // 2, True, False, n)
                        for s in range(n):
                            (si2, sj2, i2, j2) = slot_ij(units[u][k + s])
                            mx(z[:, (k + s) * P:(k + s + 1) * P], wi[i2 % 2], c, si2, i2 // 2, False, s == n - 1)
                    k += n
                nc.scalar.activation(out=hp[:, c, :], in_=z[:], func=ACT.Gelu, bias=b1f[:, c:c + 1], scale=1.0)
            hg = hpool.tile([P, UNIT * P, CH], BF16, name="hg", align_bytes=64)
            hgs[u] = hg
            n = v_cols(u)
            if n < UNIT * P:
                nc.scalar.copy(out=hg[:, n:, :].rearrange("p (c i) t -> p c t i", i=4),
                               in_=hps[u][:, :, n:].rearrange("p t (c i) -> p c t i", i=4))

        def regroup(u):
            n = v_cols(u)
            hg = hgs[u]
            nc.vector.tensor_copy(out=hg[:, 0:n, :].rearrange("p (c i) t -> p c t i", i=4),
                                  in_=hps[u][:, :, 0:n].rearrange("p t (c i) -> p c t i", i=4))

        def quant(u):
            hc = hpool.tile([P, UNIT * P], U32, name="hc", align_bytes=64)
            hs = hpool.tile([P, UNIT * P], U8, name="hs", align_bytes=64)
            nc.vector.quantize_mx(out=hc[:].bitcast(FP8X4), scales=hs[:],
                                  in_=hgs[u][:].rearrange("p r t -> p (r t)"))
            hcs[u] = (hc, hs)

        def stage2(u):
            (hc, hs) = hcs[u]
            qbs[u] = []
            for kk in range(2):
                qb = qpool.tile([P, 2, D], F32, name="qb")
                for h in range(2):
                    cols = slice((2 * kk + h) * P, (2 * kk + h + 1) * P)
                    nc.tensor.matmul_mx(out=qb[:, h, :], lhsT=hc[:, cols].bitcast(FP8X4), lhsT_scale=hs[:, cols],
                                        rhs=w2q[0][:].bitcast(FP8X4), rhs_scale=w2q[1][:], start=True, stop=True)
                qbs[u].append(qb)

        def sm_tile(bi, nm, width):
            t = keep.tile([P, 2, width], F32, name="%s_%d" % (nm, bi))
            small[(bi, nm)] = t
            return t

        def fill_one(force):
            chains = [c for c in state["chains"] if len(c["ops"]) > c["at"]]
            state["chains"] = chains
            if len(chains) == 0:
                return False
            pick = None
            for c in sorted(chains, key=lambda c: c["key"][0] == "e") if state["t"] >= SOFT_FIRST else chains:
                if c["key"] != state["last"]:
                    pick = c
                    break
            if pick is None:
                if not force:
                    return False
                pick = chains[0]
            op = pick["ops"][pick["at"]]
            pick["at"] += 1
            state["last"] = pick["key"]
            state["chains"] = [c for c in chains if c["key"] != pick["key"]] + [pick]
            op()
            return True

        def fill(n):
            done = 0
            while done < n and fill_one(False):
                done += 1
            return done

        def main_op():
            state["last"] = None

        def add_chain(key, ops):
            state["chains"].append({"key": key, "ops": ops, "at": 0})

        def e3_op(bi, rr, idx):
            def emit():
                row = batches[bi]["rows"][rr]
                aa = small[(bi, "aa")]
                (u, k) = pos[(bi, rr, idx)]
                acc = otile[row["g"]][:, row["orow"], :]
                if idx == 0:
                    nc.vector.tensor_scalar(out=acc, in0=pts[u][:, k, :], scalar1=aa[:, rr, 0:1], scalar2=None,
                                            op0=ALU.mult)
                else:
                    nc.vector.scalar_tensor_tensor(out=acc, in0=pts[u][:, k, :], scalar=aa[:, rr, idx:idx + 1],
                                                   in1=acc, op0=ALU.mult, op1=ALU.add)
                left[u] -= 1
                if idx == len(row["js"]) - 1:
                    g = row["g"]
                    if g < 2:
                        nc.sync.dma_start(out=out[g * P:(g + 1) * P, row["i"], :], in_=acc)
                    else:
                        r = row["orow"]
                        nc.sync.dma_start(out=out[2 * P:2 * P + 64, 2 * r + 1, :], in_=otile[2][0:64, r, :])
                        nc.sync.dma_start(out=out[2 * P:2 * P + 64, 2 * r, :], in_=otile[2][64:128, r, :])
            return emit

        def evac_alloc(u):
            if u - PBUFS in left:
                while left[u - PBUFS] > 0:
                    assert fill_one(True)
            pts[u] = ppool.tile([P, UNIT, D], F32, name="pt")
            left[u] = UNIT

        def evac(u, kk):
            nc.vector.tensor_tensor(out=pts[u][:, 2 * kk:2 * kk + 2, :], in0=qbs[u][kk][:], in1=b2f[:], op=ALU.add)

        def squares(u):
            for k, (bi, rr, idx) in enumerate(units[u]):
                row = batches[bi]["rows"][rr]
                if batches[bi]["direct"]:
                    g = row["g"]
                    nc.sync.dma_start(out=out[g * P:(g + 1) * P, row["i"], :], in_=pts[u][:, k, :])
                    left[u] -= 1
                    continue
                if (bi, "n2") not in small:
                    sm_tile(bi, "n2", NPOS)
                if k in (V_SQ_EARLY if u < U_EARLY else ()):
                    nc.vector.scalar_tensor_tensor(out=junk_v[:], in0=pts[u][:, k, :], scalar=0.25, in1=pts[u][:, k, :],
                                                   op0=ALU.mult, op1=ALU.mult,
                                                   accum_out=small[(bi, "n2")][:, rr, idx:idx + 1])
                    main_op()
                else:
                    nc.scalar.activation(out=junk[:], in_=pts[u][:, k, :], func=ACT.Square, scale=0.5,
                                         accum_out=small[(bi, "n2")][:, rr, idx:idx + 1])

        def dims(bi):
            return (len(batches[bi]["rows"]), len(batches[bi]["rows"][0]["js"]))

        def sm_a(bi):
            (nr, n) = dims(bi)
            nrm = sm_tile(bi, "nrm", NPOS)
            nc.gpsimd.tensor_tensor(out=nrm[:, 0:nr, 0:n], in0=small[(bi, "n2")][:, 0:nr, 0:n],
                                    in1=half[:, 0:nr, 0:n], op=ALU.pow)
            if batches[bi]["masked"]:
                nc.gpsimd.memset(nrm[64:128, 0, n - 1:n], -1e9)

        def sm_b(bi):
            (nr, n) = dims(bi)
            nrm = small[(bi, "nrm")]
            mxv = sm_tile(bi, "mx", 1)

            def op_max():
                nc.vector.tensor_reduce(out=mxv[:, 0:nr, 0], in_=nrm[:, 0:nr, 0:n], axis=AX.X, op=ALU.max)
                at = state["t"] + LAG_T
                tanh_at[at] = tanh_at.get(at, []) + [bi]

            add_chain(("b", bi), [op_max])

        def sm_t(bi):
            (nr, n) = dims(bi)
            nrm = small[(bi, "nrm")]
            mxv = small[(bi, "mx")]
            th = sm_tile(bi, "th", NPOS)
            vv = sm_tile(bi, "vv", NPOS)
            for rr in range(nr):
                nc.scalar.activation(out=th[:, rr, 0:n], in_=nrm[:, rr, 0:n], func=ACT.Tanh, bias=mxv[:, rr, 0:1],
                                     scale=-1.0)
            nc.scalar.activation(out=vv[:, 0:nr, 0:n], in_=th[:, 0:nr, 0:n], func=ACT.Identity, bias=one[:, 0:1],
                                 scale=1.0)

        def sm_c(bi):
            (nr, n) = dims(bi)
            vv = small[(bi, "vv")]
            rd = sm_tile(bi, "rd", NPOS)
            ee = sm_tile(bi, "ee", NPOS)
            sv = sm_tile(bi, "sv", 1)
            rv = sm_tile(bi, "rv", 1)
            aa = sm_tile(bi, "aa", NPOS)

            def op_rd():
                nc.vector.reciprocal(out=rd[:, 0:nr, 0:n], in_=vv[:, 0:nr, 0:n])

            def op_ee():
                nc.vector.tensor_scalar(out=ee[:, 0:nr, 0:n], in0=rd[:, 0:nr, 0:n], scalar1=2.0, scalar2=-1.0,
                                        op0=ALU.mult, op1=ALU.add)

            def op_sum():
                nc.vector.tensor_reduce(out=sv[:, 0:nr, 0], in_=ee[:, 0:nr, 0:n], axis=AX.X, op=ALU.add)

            def op_rec():
                nc.vector.reciprocal(out=rv[:, 0:nr, :], in_=sv[:, 0:nr, :])

            def op_mul():
                nc.vector.tensor_tensor(out=aa[:, 0:nr, 0:n], in0=ee[:, 0:nr, 0:n],
                                        in1=rv[:, 0:nr, :].to_broadcast([P, nr, n]), op=ALU.mult)
                first = 0
                if FIRST_ON_S <= bi < FIRST_TO:
                    first = 1
                    for rr in range(nr):
                        row = batches[bi]["rows"][rr]
                        (u, k) = pos[(bi, rr, 0)]
                        nc.scalar.activation(out=otile[row["g"]][:, row["orow"], :], in_=pts[u][:, k, :], func=ACT.Copy,
                                             scale=aa[:, rr, 0:1])
                        left[u] -= 1
                for rr in range(nr):
                    add_chain(("e", bi, rr), [e3_op(bi, rr, idx) for idx in range(first, n)])

            ops = [op_rd, op_ee, op_sum, op_rec, op_mul]
            add_chain(("c", bi), ops)

        later_x = {0: 2, 1: 3}
        for t in range(n_units + 14):
            state["t"] = t
            if t < n_units:
                stage1(t)
            for bi in tanh_at.get(t - LAG_C, []):
                sm_c(bi)
            for bi in range(len(batches)):
                if batches[bi]["direct"]:
                    continue
                if last_unit[bi] == t - (LAG_B if bi < 8 else 4):
                    sm_b(bi)
            if 0 <= t - 1 < n_units:
                regroup(t - 1)
                main_op()
            fill(GAP)
            if 0 <= t - 2 < n_units:
                evac_alloc(t - 2)
                evac(t - 2, 0)
                main_op()
            fill(GAP)
            if 0 <= t - 1 < n_units:
                quant(t - 1)
                main_op()
                stage2(t - 1)
            fill(GAP)
            if 0 <= t - 2 < n_units:
                evac(t - 2, 1)
                main_op()
            fill(GAP)
            if t - 1 in later_x:
                xprep_q(later_x[t - 1], xgl)
                main_op()
            if t in later_x:
                xgl = xprep_t(later_x[t])
                main_op()
            if 0 <= t - 3 < n_units:
                squares(t - 3)
            for bi in tanh_at.get(t, []):
                sm_t(bi)
            for bi in range(len(batches)):
                if not batches[bi]["direct"] and last_unit[bi] == t - 3:
                    sm_a(bi)
        while fill_one(True):
            pass
